import numpy as np
import ml_dtypes


def mxq(x, axis, fmt="e4m3"):
    dtype, down = {"e4m3": (ml_dtypes.float8_e4m3fn, 7), "e5m2": (ml_dtypes.float8_e5m2, 14)}[fmt]
    v = np.moveaxis(np.asarray(x, np.float32).astype(ml_dtypes.bfloat16).astype(np.float64), axis, -1)
    blocks = v.reshape(v.shape[:-1] + (-1, 32))
    amax = np.abs(blocks).max(-1, keepdims=True)
    byte = np.maximum(np.where(amax > 0, np.frexp(amax)[1] - 1 + 127, 0) - down, 1)
    scale = np.exp2(byte - 127.0)
    codes = (blocks / scale).astype(np.float32).astype(dtype).astype(np.float64)
    return np.moveaxis((codes * scale).reshape(v.shape), -1, axis)


WIDE = False


def mx_kscale(k):
    if not WIDE:
        return np.ones(k)
    levels = np.array([10, -10, 5, -5, 0])
    a = np.random.permutation(np.resize(levels, k // 512 * 4)).reshape(k // 512, 4)
    idx = np.arange(k)
    return np.exp2(a[idx // 512, idx % 128 // 32])


BF16 = ml_dtypes.bfloat16


def bf(x):
    return np.asarray(x, np.float32).astype(BF16)


def f64(x):
    return np.asarray(x).astype(np.float64)


N, S, I, L, M = 1024, 4, 512, 512, 256
D = I + L


def sigmoid(v):
    return 1.0 / (1.0 + np.exp(-v))


def setup_inputs():
    s = mx_kscale(D)
    r = np.random.standard_normal
    return {"modulation": bf((r((N, S, I)) * s[:I]).reshape(N, S * I)),
            "h0": bf((r((N, S, L)) * s[I:]).reshape(N, S * L)),
            "c_new": bf(0.75 * r((N, S * L))),
            "Wo": bf(r((S, L, D)) / np.sqrt(D) / s), "b_o": bf(0.3 * r((S, L))),
            "Wy": bf(r((S, M, L)) * 2.0 / np.sqrt(L)), "b_y": bf(0.2 * r((S, M)))}


def proj(aq, W, b):
    return (aq.transpose(1, 0, 2) @ mxq(f64(W), 2, "e4m3").transpose(0, 2, 1)).transpose(1, 0, 2) + f64(b)


def reference(modulation, h0, c_new, Wo, b_o, Wy, b_y):
    x = f64(modulation).reshape(N, S, I)
    h = f64(h0).reshape(N, S, L)
    c = f64(c_new).reshape(N, S, L)
    xq = mxq(np.concatenate([x, h], axis=-1), 2, "e4m3")
    o = sigmoid(proj(xq, Wo, b_o))
    h_new = o * np.tanh(c)
    y = proj(mxq(h_new, 2, "e4m3"), Wy, b_y)
    return y.reshape(N, S * M)

@@ -1,0 +1,341 @@
+from contextlib import ExitStack
+
+import concourse.mybir as mybir
+from concourse.masks import make_identity
+
+F32 = mybir.dt.float32
+BF16 = mybir.dt.bfloat16
+U32 = mybir.dt.uint32
+U8 = mybir.dt.uint8
+I32 = mybir.dt.int32
+FP8X4 = mybir.dt.float8_e4m3fn_x4
+ACT = mybir.ActivationFunctionType
+ALU = mybir.AluOpType
+
+P = 128
+ROWS, STREAMS, FEAT, HID, OUTF = 1024, 4, 512, 512, 256
+CHUNK = 256
+NCHUNK = ROWS // CHUNK
+UNITS = NCHUNK * STREAMS
+BANK = 512
+FINE_CHUNKS = 2
+
+FLOPS = 2 * ROWS * STREAMS * ((FEAT + HID) * HID + HID * OUTF)
+
+PINNED = False
+
+
+def preps_of(step):
+    if step < 3:
+        return [step]
+    if step == 3:
+        return [3, 4]
+    if step == 4:
+        return [5, 6]
+    if step + 2 < UNITS:
+        return [step + 2]
+    return []
+
+
+def quants_of(step):
+    if step < 4:
+        return [step]
+    if step == 4:
+        return [4, 5]
+    if step + 1 < UNITS:
+        return [step + 1]
+    return []
+
+
+def tile_flatlstm_pb_t_kernel(tc, modulation, h0, c_new, Wo, b_o, Wy, b_y, out):
+    nc = tc.nc
+    with ExitStack() as ctx:
+        const = ctx.enter_context(tc.tile_pool(name="const", bufs=1))
+        wraw = ctx.enter_context(tc.tile_pool(name="wraw", bufs=3))
+        fine = ctx.enter_context(tc.tile_pool(name="fine", bufs=4))
+        coarse = ctx.enter_context(tc.tile_pool(name="coarse", bufs=NCHUNK - FINE_CHUNKS))
+        grp2 = ctx.enter_context(tc.tile_pool(name="grp2", bufs=2))
+        grp3 = ctx.enter_context(tc.tile_pool(name="grp3", bufs=3))
+        code4 = ctx.enter_context(tc.tile_pool(name="code4", bufs=4))
+        outp = ctx.enter_context(tc.tile_pool(name="outp", bufs=2))
+        psum = ctx.enter_context(tc.psum_pool(name="psum", bufs=8))
+        if PINNED:
+            ctx.enter_context(tc.manual_schedule())
+
+        def bank(label):
+            return psum.tile([P, BANK], F32, tag="bank", name=label)
+
+        ident = const.tile([P, P], F32, name="ident")
+        make_identity(nc, ident[:])
+        ones = const.tile([P, P], BF16, name="ones")
+        nc.vector.memset(ones[:], 1.0)
+        zb = const.tile([P, STREAMS * OUTF + 256], BF16, name="zb")
+        nc.vector.memset(zb[:].bitcast(I32), 0)
+        nc.scalar.dma_start(out=zb[0:1, 0 : STREAMS * OUTF], in_=b_y.rearrange("(o s) m -> o (s m)", o=1))
+        nc.scalar.dma_start(
+            out=zb[0:8, STREAMS * OUTF : STREAMS * OUTF + 256], in_=b_o.rearrange("s (u q) -> (s u) q", u=2)
+        )
+
+        warm_in = const.tile([P, 1], F32, name="warm_in")
+        warm_out = const.tile([P, 1], F32, name="warm_out")
+        nc.vector.memset(warm_in[:], 0.0)
+        nc.scalar.activation(out=warm_out[:], in_=warm_in[:], func=ACT.Sigmoid)
+
+        wo_codes = const.tile([P, STREAMS * 1024], U32, name="wo_codes", align_bytes=64)
+        wo_plane = const.tile([P, STREAMS * 1024], U8, name="wo_plane", align_bytes=64)
+        wy_codes = const.tile([P, STREAMS * OUTF], U32, name="wy_codes", align_bytes=64)
+        wy_plane = const.tile([P, STREAMS * OUTF], U8, name="wy_plane", align_bytes=64)
+        by_b = const.tile([P, STREAMS * OUTF], F32, name="by_b")
+        bo = const.tile([P, 16], F32, name="bo")
+
+        raw = {}
+        wo_raw = {}
+        wy_raw = {}
+        srcs = {"x": modulation, "h": h0, "c": c_new}
+
+        def load_fine(kind, unit):
+            k, s = unit // STREAMS, unit % STREAMS
+            t = fine.tile([P, 2 * FEAT], BF16, tag="fine_" + kind, name="fine_" + kind)
+            nc.sync.dma_start(
+                out=t[:].rearrange("p (j d) -> p j d", j=2),
+                in_=srcs[kind][k * CHUNK : (k + 1) * CHUNK, s * FEAT : (s + 1) * FEAT].rearrange(
+                    "(p j) d -> p j d", j=2
+                ),
+            )
+            raw[(kind, unit)] = (t[:].bitcast(F32), 0, FEAT // 2)
+
+        def load_coarse(kind, k):
+            t = coarse.tile([P, 2 * STREAMS * FEAT], BF16, tag="coarse_" + kind, name="coarse_" + kind)
+            nc.sync.dma_start(
+                out=t[:], in_=srcs[kind][k * CHUNK : (k + 1) * CHUNK, :].rearrange("(p j) d -> p (j d)", j=2)
+            )
+            for s in range(STREAMS):
+                raw[(kind, k * STREAMS + s)] = (t[:].bitcast(F32), s * (FEAT // 2), STREAMS * FEAT // 2)
+
+        def load_weights(s):
+            t = wraw.tile([P, 4096], BF16, tag="wo_raw", name="wo_raw")
+            nc.sync.dma_start(
+                out=t[:].rearrange("p (u f) -> p u f", u=2),
+                in_=Wo[s].rearrange("(u p e) d -> p u (e d)", u=2, e=2),
+            )
+            wo_raw[s] = t[:].bitcast(F32)
+            t2 = wraw.tile([P, 1024], BF16, tag="wy_raw", name="wy_raw")
+            nc.sync.dma_start(out=t2[:], in_=Wy[s].rearrange("(pm jm) l -> pm (jm l)", jm=2))
+            wy_raw[s] = t2[:].bitcast(F32)
+
+        def emit_load(n):
+            if n < FINE_CHUNKS * STREAMS:
+                load_fine("x", n)
+                load_fine("h", n)
+                if n < STREAMS:
+                    load_weights(n)
+                load_fine("c", n)
+            elif n < FINE_CHUNKS * STREAMS + NCHUNK - FINE_CHUNKS:
+                k = n - FINE_CHUNKS * STREAMS + FINE_CHUNKS
+                load_coarse("c", k)
+                load_coarse("x", k)
+                load_coarse("h", k)
+
+        def transpose4(dst, views):
+            for q, v in enumerate(views):
+                nc.tensor.transpose(dst[:, q * P : (q + 1) * P], v, ident[:])
+
+        def pair_out(on_scalar, dst_words, src):
+            o = dst_words.rearrange("p (n u) -> p n u", u=2)
+            i = src[:].rearrange("p (u n) -> p n u", u=2)
+            if on_scalar:
+                nc.scalar.copy(out=o, in_=i)
+            else:
+                nc.vector.tensor_copy(out=o, in_=i)
+
+        def act_views(kind, unit):
+            w, base, jstep = raw[(kind, unit)]
+            return [
+                w[:, base + j * jstep + u * P : base + j * jstep + (u + 1) * P] for u in range(2) for j in range(2)
+            ]
+
+        gx = {}
+        gw = {}
+        gwy = {}
+        xc = {}
+        tanh_c = {}
+        hcodes = {}
+        gate = {}
+        ybank = {}
+        out_sb = {}
+
+        def prep(unit):
+            s = unit % STREAMS
+            bx = bank("bx")
+            transpose4(bx, act_views("x", unit))
+            bh = bank("bh")
+            transpose4(bh, act_views("h", unit))
+            g = grp3.tile([P, 2048], BF16, tag="gx", name="gx", align_bytes=64)
+            gwords = g[:].bitcast(F32)
+            pair_out(True, gwords[:, 0:512], bx)
+            pair_out(False, gwords[:, 512:1024], bh)
+            gx[unit] = g
+            if unit < STREAMS:
+                ww = wo_raw[s]
+                gwt = grp2.tile([P, 4096], BF16, tag="gw", name="gw", align_bytes=64)
+                gww = gwt[:].bitcast(F32)
+                for g_ in range(2):
+                    for u in range(2):
+                        bw = bank("bw")
+                        transpose4(
+                            bw,
+                            [
+                                ww[:, u * 1024 + e * 512 + g_ * 256 + u2 * P : u * 1024 + e * 512 + g_ * 256 + (u2 + 1) * P]
+                                for u2 in range(2)
+                                for e in range(2)
+                            ],
+                        )
+                        pair_out(True, gww[:, (g_ * 2 + u) * 512 : (g_ * 2 + u + 1) * 512], bw)
+                gw[s] = gwt
+                wyw = wy_raw[s]
+                by = bank("bwy")
+                transpose4(by, [wyw[:, jm * 256 + u * P : jm * 256 + (u + 1) * P] for u in range(2) for jm in range(2)])
+                gyt = grp2.tile([P, 1024], BF16, tag="gwy", name="gwy", align_bytes=64)
+                nc.vector.tensor_copy(
+                    out=gyt[:].bitcast(F32).rearrange("p (pm jm u) -> p pm jm u", jm=2, u=2),
+                    in_=by[:].rearrange("p (u jm pm) -> p pm jm u", u=2, jm=2),
+                )
+                gwy[s] = gyt
+            bc = bank("bc")
+            transpose4(bc, act_views("c", unit))
+            t = code4.tile([P, 1024], F32, tag="tanh", name="tanh")
+            nc.scalar.activation(
+                out=t[:].rearrange("p (n u e) -> p n u e", u=2, e=2),
+                in_=bc[:].bitcast(BF16).rearrange("p (u n e) -> p n u e", u=2, e=2),
+                func=ACT.Tanh,
+            )
+            tanh_c[unit] = t
+
+        def quant(unit):
+            s = unit % STREAMS
+            codes = code4.tile([P, 512], U32, tag="xc", name="xc", align_bytes=64)
+            plane = code4.tile([P, 512], U8, tag="xp", name="xp", align_bytes=64)
+            nc.vector.quantize_mx(out=codes[:].bitcast(FP8X4), scales=plane[:], in_=gx[unit][:])
+            xc[unit] = (codes, plane)
+            if unit < STREAMS:
+                nc.vector.quantize_mx(
+                    out=wo_codes[:, s * 1024 : (s + 1) * 1024].bitcast(FP8X4),
+                    scales=wo_plane[:, s * 1024 : (s + 1) * 1024],
+                    in_=gw[s][:],
+                )
+                nc.vector.quantize_mx(
+                    out=wy_codes[:, s * OUTF : (s + 1) * OUTF].bitcast(FP8X4),
+                    scales=wy_plane[:, s * OUTF : (s + 1) * OUTF],
+                    in_=gwy[s][:],
+                )
+
+        def stage1(unit):
+            s = unit % STREAMS
+            codes, plane = xc[unit]
+            o = grp3.tile([P, 1024], F32, tag="gate", name="gate")
+            for u in range(2):
+                z = bank("z")
+                for e in range(2):
+                    for g_ in range(2):
+                        col = s * 1024 + ((g_ * 2 + u) * 2 + e) * P
+                        nc.tensor.matmul_mx(
+                            out=z[:, e * CHUNK : (e + 1) * CHUNK],
+                            lhsT=wo_codes[:, col : col + P].bitcast(FP8X4),
+                            lhsT_scale=wo_plane[:, col : col + P],
+                            rhs=codes[:, g_ * CHUNK : (g_ + 1) * CHUNK].bitcast(FP8X4),
+                            rhs_scale=plane[:, g_ * CHUNK : (g_ + 1) * CHUNK],
+                            start=(g_ == 0),
+                            stop=(g_ == 1),
+                        )
+                for e in range(2):
+                    tt = u * 2 + e
+                    nc.scalar.activation(
+                        out=o[:, tt * CHUNK : (tt + 1) * CHUNK],
+                        in_=z[:, e * CHUNK : (e + 1) * CHUNK],
+                        func=ACT.Sigmoid,
+                        bias=bo[:, s * 4 + tt : s * 4 + tt + 1],
+                    )
+            gate[unit] = o
+
+        hgs = {}
+
+        def multiply(unit):
+            hg = grp3.tile([P, 1024], BF16, tag="hg", name="hg", align_bytes=64)
+            nc.vector.tensor_tensor(
+                out=hg[:].rearrange("p (n t) -> p n t", t=4),
+                in0=gate[unit][:].rearrange("p (t n) -> p n t", t=4),
+                in1=tanh_c[unit][:].rearrange("p (n t) -> p n t", t=4),
+                op=ALU.mult,
+            )
+            hgs[unit] = hg
+
+        def quant_h(unit):
+            codes = grp3.tile([P, CHUNK], U32, tag="hc", name="hc", align_bytes=64)
+            plane = grp3.tile([P, CHUNK], U8, tag="hp", name="hp", align_bytes=64)
+            nc.vector.quantize_mx(out=codes[:].bitcast(FP8X4), scales=plane[:], in_=hgs[unit][:])
+            hcodes[unit] = (codes, plane)
+
+        def stage2(unit):
+            s = unit % STREAMS
+            codes, plane = hcodes[unit]
+            y = bank("y")
+            for j in range(2):
+                nc.tensor.matmul_mx(
+                    out=y[:, j * OUTF : (j + 1) * OUTF],
+                    lhsT=codes[:, j * P : (j + 1) * P].bitcast(FP8X4),
+                    lhsT_scale=plane[:, j * P : (j + 1) * P],
+                    rhs=wy_codes[:, s * OUTF : (s + 1) * OUTF].bitcast(FP8X4),
+                    rhs_scale=wy_plane[:, s * OUTF : (s + 1) * OUTF],
+                    start=True,
+                    stop=True,
+                )
+            ybank[unit] = y
+
+        def add_bias(unit):
+            k, s = unit // STREAMS, unit % STREAMS
+            if s == 0:
+                out_sb[k] = outp.tile([P, 2 * STREAMS * OUTF], F32, tag="out_sb", name="out_sb")
+            nc.vector.tensor_tensor(
+                out=out_sb[k][:].rearrange("p (j m) -> p j m", j=2)[:, :, s * OUTF : (s + 1) * OUTF],
+                in0=ybank[unit][:].rearrange("p (j m) -> p j m", j=2),
+                in1=by_b[:, s * OUTF : (s + 1) * OUTF].unsqueeze(1).to_broadcast([P, 2, OUTF]),
+                op=ALU.add,
+            )
+            if s == STREAMS - 1:
+                nc.sync.dma_start(
+                    out=out[k * CHUNK : (k + 1) * CHUNK, :].rearrange("(p j) m -> p (j m)", j=2), in_=out_sb[k][:]
+                )
+
+        for n in range(3):
+            emit_load(n)
+        next_load = [3]
+
+        for c in range(2):
+            pb = bank("pb")
+            nc.tensor.matmul(out=pb[:], lhsT=ones[:], rhs=zb[:, c * BANK : (c + 1) * BANK], start=True, stop=True)
+            nc.vector.tensor_copy(out=by_b[:, c * BANK : (c + 1) * BANK], in_=pb[:])
+        pbo = bank("pbo")
+        nc.tensor.transpose(pbo[:, 0:P], zb[:, STREAMS * OUTF : STREAMS * OUTF + 256].bitcast(F32), ident[:])
+        nc.vector.tensor_copy(out=bo[:], in_=pbo[:, 0:8].bitcast(BF16))
+
+        for step in range(UNITS + 2):
+            for a in preps_of(step):
+                prep(a)
+                emit_load(next_load[0])
+                next_load[0] = next_load[0] + 1
+                if a == 4:
+                    for extra in range(3):
+                        emit_load(next_load[0])
+                        next_load[0] = next_load[0] + 1
+            if 0 <= step - 2 < UNITS:
+                add_bias(step - 2)
+            if 0 <= step - 1 < UNITS:
+                multiply(step - 1)
+            for a in quants_of(step):
+                quant(a)
+            if 0 <= step - 1 < UNITS:
+                quant_h(step - 1)
+            if step < UNITS:
+                stage1(step)
+            if 0 <= step - 1 < UNITS:
+                stage2(step - 1)

@@ -18,46 +18,27 @@ CHUNK = 256
 NCHUNK = ROWS // CHUNK
 UNITS = NCHUNK * STREAMS
 BANK = 512
-FINE_CHUNKS = 2
 
 FLOPS = 2 * ROWS * STREAMS * ((FEAT + HID) * HID + HID * OUTF)
 
-PINNED = False
-
-
-def preps_of(step):
-    if step < 3:
-        return [step]
-    if step == 3:
-        return [3, 4]
-    if step == 4:
-        return [5, 6]
-    if step + 2 < UNITS:
-        return [step + 2]
-    return []
-
-
-def quants_of(step):
-    if step < 4:
-        return [step]
-    if step == 4:
-        return [4, 5]
-    if step + 1 < UNITS:
-        return [step + 1]
-    return []
+PINNED = True
+PREFETCH = 6
+H_ON_SCALAR = (5, 9, 13)
+W0_ON_VECTOR = (1, 3)
+W_STEPS = ((), (0, 1), (2, 3, "y"), ("Q", "QY"))
+M2_LAG = 2
+ADD_LAG = 3
 
 
 def tile_flatlstm_pb_t_kernel(tc, modulation, h0, c_new, Wo, b_o, Wy, b_y, out):
     nc = tc.nc
     with ExitStack() as ctx:
         const = ctx.enter_context(tc.tile_pool(name="const", bufs=1))
-        wraw = ctx.enter_context(tc.tile_pool(name="wraw", bufs=3))
-        fine = ctx.enter_context(tc.tile_pool(name="fine", bufs=4))
-        coarse = ctx.enter_context(tc.tile_pool(name="coarse", bufs=NCHUNK - FINE_CHUNKS))
+        wraw = ctx.enter_context(tc.tile_pool(name="wraw", bufs=2))
+        fine = ctx.enter_context(tc.tile_pool(name="fine", bufs=8))
         grp2 = ctx.enter_context(tc.tile_pool(name="grp2", bufs=2))
         grp3 = ctx.enter_context(tc.tile_pool(name="grp3", bufs=3))
-        code4 = ctx.enter_context(tc.tile_pool(name="code4", bufs=4))
-        outp = ctx.enter_context(tc.tile_pool(name="outp", bufs=2))
+        grp4 = ctx.enter_context(tc.tile_pool(name="grp4", bufs=4))
         psum = ctx.enter_context(tc.psum_pool(name="psum", bufs=8))
         if PINNED:
             ctx.enter_context(tc.manual_schedule())
@@ -65,21 +46,20 @@ def tile_flatlstm_pb_t_kernel(tc, modulation, h0, c_new, Wo, b_o, Wy, b_y, out):
         def bank(label):
             return psum.tile([P, BANK], F32, tag="bank", name=label)
 
-        ident = const.tile([P, P], F32, name="ident")
-        make_identity(nc, ident[:])
-        ones = const.tile([P, P], BF16, name="ones")
-        nc.vector.memset(ones[:], 1.0)
         zb = const.tile([P, STREAMS * OUTF + 256], BF16, name="zb")
         nc.vector.memset(zb[:].bitcast(I32), 0)
         nc.scalar.dma_start(out=zb[0:1, 0 : STREAMS * OUTF], in_=b_y.rearrange("(o s) m -> o (s m)", o=1))
         nc.scalar.dma_start(
             out=zb[0:8, STREAMS * OUTF : STREAMS * OUTF + 256], in_=b_o.rearrange("s (u q) -> (s u) q", u=2)
         )
-
         warm_in = const.tile([P, 1], F32, name="warm_in")
         warm_out = const.tile([P, 1], F32, name="warm_out")
         nc.vector.memset(warm_in[:], 0.0)
         nc.scalar.activation(out=warm_out[:], in_=warm_in[:], func=ACT.Sigmoid)
+        ident = const.tile([P, P], F32, name="ident")
+        make_identity(nc, ident[:])
+        ones = const.tile([P, P], BF16, name="ones")
+        nc.vector.memset(ones[:], 1.0)
 
         wo_codes = const.tile([P, STREAMS * 1024], U32, name="wo_codes", align_bytes=64)
         wo_plane = const.tile([P, STREAMS * 1024], U8, name="wo_plane", align_bytes=64)
@@ -94,7 +74,7 @@ def tile_flatlstm_pb_t_kernel(tc, modulation, h0, c_new, Wo, b_o, Wy, b_y, out):
         srcs = {"x": modulation, "h": h0, "c": c_new}
 
         def load_fine(kind, unit):
-            k, s = unit // STREAMS, unit % STREAMS
+            s, k = unit // NCHUNK, unit % NCHUNK
             t = fine.tile([P, 2 * FEAT], BF16, tag="fine_" + kind, name="fine_" + kind)
             nc.sync.dma_start(
                 out=t[:].rearrange("p (j d) -> p j d", j=2),
@@ -102,39 +82,28 @@ def tile_flatlstm_pb_t_kernel(tc, modulation, h0, c_new, Wo, b_o, Wy, b_y, out):
                     "(p j) d -> p j d", j=2
                 ),
             )
-            raw[(kind, unit)] = (t[:].bitcast(F32), 0, FEAT // 2)
-
-        def load_coarse(kind, k):
-            t = coarse.tile([P, 2 * STREAMS * FEAT], BF16, tag="coarse_" + kind, name="coarse_" + kind)
-            nc.sync.dma_start(
-                out=t[:], in_=srcs[kind][k * CHUNK : (k + 1) * CHUNK, :].rearrange("(p j) d -> p (j d)", j=2)
-            )
-            for s in range(STREAMS):
-                raw[(kind, k * STREAMS + s)] = (t[:].bitcast(F32), s * (FEAT // 2), STREAMS * FEAT // 2)
+            raw[(kind, unit)] = t[:].bitcast(F32)
 
         def load_weights(s):
             t = wraw.tile([P, 4096], BF16, tag="wo_raw", name="wo_raw")
-            nc.sync.dma_start(
-                out=t[:].rearrange("p (u f) -> p u f", u=2),
-                in_=Wo[s].rearrange("(u p e) d -> p u (e d)", u=2, e=2),
-            )
+            for u in range(2):
+                nc.sync.dma_start(
+                    out=t[:, u * 2048 : (u + 1) * 2048],
+                    in_=Wo[s][u * 256 : (u + 1) * 256, :].rearrange("(p e) d -> p (e d)", e=2),
+                )
             wo_raw[s] = t[:].bitcast(F32)
             t2 = wraw.tile([P, 1024], BF16, tag="wy_raw", name="wy_raw")
             nc.sync.dma_start(out=t2[:], in_=Wy[s].rearrange("(pm jm) l -> pm (jm l)", jm=2))
             wy_raw[s] = t2[:].bitcast(F32)
 
-        def emit_load(n):
-            if n < FINE_CHUNKS * STREAMS:
-                load_fine("x", n)
-                load_fine("h", n)
-                if n < STREAMS:
-                    load_weights(n)
-                load_fine("c", n)
-            elif n < FINE_CHUNKS * STREAMS + NCHUNK - FINE_CHUNKS:
-                k = n - FINE_CHUNKS * STREAMS + FINE_CHUNKS
-                load_coarse("c", k)
-                load_coarse("x", k)
-                load_coarse("h", k)
+        def load_unit(n):
+            if n >= UNITS:
+                return
+            if n % NCHUNK == NCHUNK - 1 and n // NCHUNK + 1 < STREAMS:
+                load_weights(n // NCHUNK + 1)
+            load_fine("x", n)
+            load_fine("h", n)
+            load_fine("c", n)
 
         def transpose4(dst, views):
             for q, v in enumerate(views):
@@ -148,11 +117,11 @@ def tile_flatlstm_pb_t_kernel(tc, modulation, h0, c_new, Wo, b_o, Wy, b_y, out):
             else:
                 nc.vector.tensor_copy(out=o, in_=i)
 
-        def act_views(kind, unit):
-            w, base, jstep = raw[(kind, unit)]
-            return [
-                w[:, base + j * jstep + u * P : base + j * jstep + (u + 1) * P] for u in range(2) for j in range(2)
-            ]
+        def act_bank(kind, unit):
+            w = raw[(kind, unit)]
+            b = bank("b" + kind)
+            transpose4(b, [w[:, j * 256 + u * P : j * 256 + (u + 1) * P] for u in range(2) for j in range(2)])
+            return b
 
         gx = {}
         gw = {}
@@ -161,37 +130,12 @@ def tile_flatlstm_pb_t_kernel(tc, modulation, h0, c_new, Wo, b_o, Wy, b_y, out):
         tanh_c = {}
         hcodes = {}
         gate = {}
+        hgs = {}
         ybank = {}
-        out_sb = {}
+        hbank = {}
 
-        def prep(unit):
-            s = unit % STREAMS
-            bx = bank("bx")
-            transpose4(bx, act_views("x", unit))
-            bh = bank("bh")
-            transpose4(bh, act_views("h", unit))
-            g = grp3.tile([P, 2048], BF16, tag="gx", name="gx", align_bytes=64)
-            gwords = g[:].bitcast(F32)
-            pair_out(True, gwords[:, 0:512], bx)
-            pair_out(False, gwords[:, 512:1024], bh)
-            gx[unit] = g
-            if unit < STREAMS:
-                ww = wo_raw[s]
-                gwt = grp2.tile([P, 4096], BF16, tag="gw", name="gw", align_bytes=64)
-                gww = gwt[:].bitcast(F32)
-                for g_ in range(2):
-                    for u in range(2):
-                        bw = bank("bw")
-                        transpose4(
-                            bw,
-                            [
-                                ww[:, u * 1024 + e * 512 + g_ * 256 + u2 * P : u * 1024 + e * 512 + g_ * 256 + (u2 + 1) * P]
-                                for u2 in range(2)
-                                for e in range(2)
-                            ],
-                        )
-                        pair_out(True, gww[:, (g_ * 2 + u) * 512 : (g_ * 2 + u + 1) * 512], bw)
-                gw[s] = gwt
+        def weight_piece(s, piece):
+            if piece == "y":
                 wyw = wy_raw[s]
                 by = bank("bwy")
                 transpose4(by, [wyw[:, jm * 256 + u * P : jm * 256 + (u + 1) * P] for u in range(2) for jm in range(2)])
@@ -201,9 +145,42 @@ def tile_flatlstm_pb_t_kernel(tc, modulation, h0, c_new, Wo, b_o, Wy, b_y, out):
                     in_=by[:].rearrange("p (u jm pm) -> p pm jm u", u=2, jm=2),
                 )
                 gwy[s] = gyt
-            bc = bank("bc")
-            transpose4(bc, act_views("c", unit))
-            t = code4.tile([P, 1024], F32, tag="tanh", name="tanh")
+            elif piece == "Q":
+                nc.vector.quantize_mx(
+                    out=wo_codes[:, s * 1024 : (s + 1) * 1024].bitcast(FP8X4),
+                    scales=wo_plane[:, s * 1024 : (s + 1) * 1024],
+                    in_=gw[s][:],
+                )
+            elif piece == "QY":
+                nc.vector.quantize_mx(
+                    out=wy_codes[:, s * OUTF : (s + 1) * OUTF].bitcast(FP8X4),
+                    scales=wy_plane[:, s * OUTF : (s + 1) * OUTF],
+                    in_=gwy[s][:],
+                )
+            else:
+                u, g_ = piece // 2, piece % 2
+                if piece == 0:
+                    gw[s] = grp2.tile([P, 4096], BF16, tag="gw", name="gw", align_bytes=64)
+                ww = wo_raw[s]
+                bw = bank("bw")
+                transpose4(
+                    bw,
+                    [
+                        ww[:, u * 1024 + e * 512 + g_ * 256 + u2 * P : u * 1024 + e * 512 + g_ * 256 + (u2 + 1) * P]
+                        for u2 in range(2)
+                        for e in range(2)
+                    ],
+                )
+                on_scalar = not (s == 0 and piece in W0_ON_VECTOR)
+                pair_out(on_scalar, gw[s][:].bitcast(F32)[:, (g_ * 2 + u) * 512 : (g_ * 2 + u + 1) * 512], bw)
+
+        def prep_front(unit):
+            bx = act_bank("x", unit)
+            hbank[unit] = act_bank("h", unit)
+            bc = act_bank("c", unit)
+            gx[unit] = grp3.tile([P, 2048], BF16, tag="gx", name="gx", align_bytes=64)
+            pair_out(True, gx[unit][:].bitcast(F32)[:, 0:512], bx)
+            t = grp4.tile([P, 1024], F32, tag="tanh", name="tanh")
             nc.scalar.activation(
                 out=t[:].rearrange("p (n u e) -> p n u e", u=2, e=2),
                 in_=bc[:].bitcast(BF16).rearrange("p (u n e) -> p n u e", u=2, e=2),
@@ -211,26 +188,17 @@ def tile_flatlstm_pb_t_kernel(tc, modulation, h0, c_new, Wo, b_o, Wy, b_y, out):
             )
             tanh_c[unit] = t
 
-        def quant(unit):
-            s = unit % STREAMS
-            codes = code4.tile([P, 512], U32, tag="xc", name="xc", align_bytes=64)
-            plane = code4.tile([P, 512], U8, tag="xp", name="xp", align_bytes=64)
+        def prep_h(unit):
+            pair_out(unit in H_ON_SCALAR, gx[unit][:].bitcast(F32)[:, 512:1024], hbank[unit])
+
+        def quant_x(unit):
+            codes = grp3.tile([P, 512], U32, tag="xc", name="xc", align_bytes=64)
+            plane = grp3.tile([P, 512], U8, tag="xp", name="xp", align_bytes=64)
             nc.vector.quantize_mx(out=codes[:].bitcast(FP8X4), scales=plane[:], in_=gx[unit][:])
             xc[unit] = (codes, plane)
-            if unit < STREAMS:
-                nc.vector.quantize_mx(
-                    out=wo_codes[:, s * 1024 : (s + 1) * 1024].bitcast(FP8X4),
-                    scales=wo_plane[:, s * 1024 : (s + 1) * 1024],
-                    in_=gw[s][:],
-                )
-                nc.vector.quantize_mx(
-                    out=wy_codes[:, s * OUTF : (s + 1) * OUTF].bitcast(FP8X4),
-                    scales=wy_plane[:, s * OUTF : (s + 1) * OUTF],
-                    in_=gwy[s][:],
-                )
 
         def stage1(unit):
-            s = unit % STREAMS
+            s = unit // NCHUNK
             codes, plane = xc[unit]
             o = grp3.tile([P, 1024], F32, tag="gate", name="gate")
             for u in range(2):
@@ -257,8 +225,6 @@ def tile_flatlstm_pb_t_kernel(tc, modulation, h0, c_new, Wo, b_o, Wy, b_y, out):
                     )
             gate[unit] = o
 
-        hgs = {}
-
         def multiply(unit):
             hg = grp3.tile([P, 1024], BF16, tag="hg", name="hg", align_bytes=64)
             nc.vector.tensor_tensor(
@@ -276,7 +242,7 @@ def tile_flatlstm_pb_t_kernel(tc, modulation, h0, c_new, Wo, b_o, Wy, b_y, out):
             hcodes[unit] = (codes, plane)
 
         def stage2(unit):
-            s = unit % STREAMS
+            s = unit // NCHUNK
             codes, plane = hcodes[unit]
             y = bank("y")
             for j in range(2):
@@ -291,51 +257,66 @@ def tile_flatlstm_pb_t_kernel(tc, modulation, h0, c_new, Wo, b_o, Wy, b_y, out):
                 )
             ybank[unit] = y
 
-        def add_bias(unit):
-            k, s = unit // STREAMS, unit % STREAMS
-            if s == 0:
-                out_sb[k] = outp.tile([P, 2 * STREAMS * OUTF], F32, tag="out_sb", name="out_sb")
+        def add_bias_and_store(unit):
+            s, k = unit // NCHUNK, unit % NCHUNK
+            res = grp4.tile([P, 2 * OUTF], F32, tag="res", name="res")
             nc.vector.tensor_tensor(
-                out=out_sb[k][:].rearrange("p (j m) -> p j m", j=2)[:, :, s * OUTF : (s + 1) * OUTF],
+                out=res[:].rearrange("p (j m) -> p j m", j=2),
                 in0=ybank[unit][:].rearrange("p (j m) -> p j m", j=2),
                 in1=by_b[:, s * OUTF : (s + 1) * OUTF].unsqueeze(1).to_broadcast([P, 2, OUTF]),
                 op=ALU.add,
             )
-            if s == STREAMS - 1:
-                nc.sync.dma_start(
-                    out=out[k * CHUNK : (k + 1) * CHUNK, :].rearrange("(p j) m -> p (j m)", j=2), in_=out_sb[k][:]
-                )
+            nc.sync.dma_start(
+                out=out[k * CHUNK : (k + 1) * CHUNK, s * OUTF : (s + 1) * OUTF].rearrange("(p j) m -> p j m", j=2),
+                in_=res[:].rearrange("p (j m) -> p j m", j=2),
+            )
 
-        for n in range(3):
-            emit_load(n)
-        next_load = [3]
+        def biases():
+            for c in range(2):
+                pb = bank("pb")
+                nc.tensor.matmul(out=pb[:], lhsT=ones[:], rhs=zb[:, c * BANK : (c + 1) * BANK], start=True, stop=True)
+                nc.vector.tensor_copy(out=by_b[:, c * BANK : (c + 1) * BANK], in_=pb[:])
+            pbo = bank("pbo")
+            nc.tensor.transpose(pbo[:, 0:P], zb[:, STREAMS * OUTF : STREAMS * OUTF + 256].bitcast(F32), ident[:])
+            nc.vector.tensor_copy(out=bo[:], in_=pbo[:, 0:8].bitcast(BF16))
 
-        for c in range(2):
-            pb = bank("pb")
-            nc.tensor.matmul(out=pb[:], lhsT=ones[:], rhs=zb[:, c * BANK : (c + 1) * BANK], start=True, stop=True)
-            nc.vector.tensor_copy(out=by_b[:, c * BANK : (c + 1) * BANK], in_=pb[:])
-        pbo = bank("pbo")
-        nc.tensor.transpose(pbo[:, 0:P], zb[:, STREAMS * OUTF : STREAMS * OUTF + 256].bitcast(F32), ident[:])
-        nc.vector.tensor_copy(out=bo[:], in_=pbo[:, 0:8].bitcast(BF16))
+        load_weights(0)
+        for n in range(PREFETCH):
+            load_unit(n)
+        next_load = [PREFETCH]
 
-        for step in range(UNITS + 2):
-            for a in preps_of(step):
-                prep(a)
-                emit_load(next_load[0])
-                next_load[0] = next_load[0] + 1
-                if a == 4:
-                    for extra in range(3):
-                        emit_load(next_load[0])
-                        next_load[0] = next_load[0] + 1
-            if 0 <= step - 2 < UNITS:
-                add_bias(step - 2)
+        weight_piece(0, 0)
+        weight_piece(0, 1)
+        biases()
+        weight_piece(0, 2)
+        weight_piece(0, 3)
+        weight_piece(0, "y")
+
+        for step in range(-1, UNITS + ADD_LAG):
+            a = step + 1
+            if a < UNITS:
+                prep_front(a)
+            if step == -1:
+                weight_piece(0, "Q")
+            if 0 <= step - ADD_LAG:
+                add_bias_and_store(step - ADD_LAG)
             if 0 <= step - 1 < UNITS:
                 multiply(step - 1)
-            for a in quants_of(step):
-                quant(a)
+            if a < UNITS:
+                prep_h(a)
+            if step == -1:
+                weight_piece(0, "QY")
             if 0 <= step - 1 < UNITS:
                 quant_h(step - 1)
-            if step < UNITS:
+            if a < UNITS:
+                quant_x(a)
+            if 0 <= step < UNITS - NCHUNK:
+                for piece in W_STEPS[step % NCHUNK]:
+                    weight_piece(step // NCHUNK + 1, piece)
+            if a < UNITS:
+                load_unit(next_load[0])
+                next_load[0] = next_load[0] + 1
+            if 0 <= step < UNITS:
                 stage1(step)
-            if 0 <= step - 1 < UNITS:
-                stage2(step - 1)
+            if 0 <= step - M2_LAG < UNITS:
+                stage2(step - M2_LAG)

@@ -182,8 +182,8 @@ def tile_flatlstm_pb_t_kernel(tc, modulation, h0, c_new, Wo, b_o, Wy, b_y, out):
             pair_out(True, gx[unit][:].bitcast(F32)[:, 0:512], bx)
             t = grp4.tile([P, 1024], F32, tag="tanh", name="tanh")
             nc.scalar.activation(
-                out=t[:].rearrange("p (n u e) -> p n u e", u=2, e=2),
-                in_=bc[:].bitcast(BF16).rearrange("p (u n e) -> p n u e", u=2, e=2),
+                out=t[:].rearrange("p (u e n) -> p u e n", u=2, e=2),
+                in_=bc[:].bitcast(BF16).rearrange("p (u n e) -> p u e n", u=2, e=2),
                 func=ACT.Tanh,
             )
             tanh_c[unit] = t
@@ -228,9 +228,9 @@ def tile_flatlstm_pb_t_kernel(tc, modulation, h0, c_new, Wo, b_o, Wy, b_y, out):
         def multiply(unit):
             hg = grp3.tile([P, 1024], BF16, tag="hg", name="hg", align_bytes=64)
             nc.vector.tensor_tensor(
-                out=hg[:].rearrange("p (n t) -> p n t", t=4),
-                in0=gate[unit][:].rearrange("p (t n) -> p n t", t=4),
-                in1=tanh_c[unit][:].rearrange("p (n t) -> p n t", t=4),
+                out=hg[:].rearrange("p (c i t) -> p c t i", i=4, t=4),
+                in0=gate[unit][:].rearrange("p (t c i) -> p c t i", t=4, i=4),
+                in1=tanh_c[unit][:].rearrange("p (t c i) -> p c t i", t=4, i=4),
                 op=ALU.mult,
             )
             hgs[unit] = hg

@@ -25,7 +25,9 @@ PINNED = True
 PREFETCH = 6
 H_ON_SCALAR = (5, 9, 13)
 W0_ON_VECTOR = (1, 3)
-W_STEPS = ((), (0, 1), (2, 3, "y"), ("Q", "QY"))
+W1_ON_VECTOR = (2,)
+W_STEPS_FIRST = ((), (), (0, 1, 2), (3, "y", "Q0", "Q1", "QY"))
+W_STEPS = ((0,), (1, "Q0"), (2, "y"), (3, "Q1", "QY"))
 M2_LAG = 2
 ADD_LAG = 3
 
@@ -84,7 +86,7 @@ def tile_flatlstm_pb_t_kernel(tc, modulation, h0, c_new, Wo, b_o, Wy, b_y, out):
             )
             raw[(kind, unit)] = t[:].bitcast(F32)
 
-        def load_weights(s):
+        def load_weights_wo(s):
             t = wraw.tile([P, 4096], BF16, tag="wo_raw", name="wo_raw")
             for u in range(2):
                 nc.sync.dma_start(
@@ -92,6 +94,8 @@ def tile_flatlstm_pb_t_kernel(tc, modulation, h0, c_new, Wo, b_o, Wy, b_y, out):
                     in_=Wo[s][u * 256 : (u + 1) * 256, :].rearrange("(p e) d -> p (e d)", e=2),
                 )
             wo_raw[s] = t[:].bitcast(F32)
+
+        def load_weights_wy(s):
             t2 = wraw.tile([P, 1024], BF16, tag="wy_raw", name="wy_raw")
             nc.sync.dma_start(out=t2[:], in_=Wy[s].rearrange("(pm jm) l -> pm (jm l)", jm=2))
             wy_raw[s] = t2[:].bitcast(F32)
@@ -100,7 +104,8 @@ def tile_flatlstm_pb_t_kernel(tc, modulation, h0, c_new, Wo, b_o, Wy, b_y, out):
             if n >= UNITS:
                 return
             if n % NCHUNK == NCHUNK - 1 and n // NCHUNK + 1 < STREAMS:
-                load_weights(n // NCHUNK + 1)
+                load_weights_wo(n // NCHUNK + 1)
+                load_weights_wy(n // NCHUNK + 1)
             load_fine("x", n)
             load_fine("h", n)
             load_fine("c", n)
@@ -145,11 +150,13 @@ def tile_flatlstm_pb_t_kernel(tc, modulation, h0, c_new, Wo, b_o, Wy, b_y, out):
                     in_=by[:].rearrange("p (u jm pm) -> p pm jm u", u=2, jm=2),
                 )
                 gwy[s] = gyt
-            elif piece == "Q":
+            elif piece == "Q0" or piece == "Q1":
+                u = 0 if piece == "Q0" else 1
+                lo = s * 1024 + u * 512
                 nc.vector.quantize_mx(
-                    out=wo_codes[:, s * 1024 : (s + 1) * 1024].bitcast(FP8X4),
-                    scales=wo_plane[:, s * 1024 : (s + 1) * 1024],
-                    in_=gw[s][:],
+                    out=wo_codes[:, lo : lo + 512].bitcast(FP8X4),
+                    scales=wo_plane[:, lo : lo + 512],
+                    in_=gw[s][:, u * 2048 : (u + 1) * 2048],
                 )
             elif piece == "QY":
                 nc.vector.quantize_mx(
@@ -171,15 +178,19 @@ def tile_flatlstm_pb_t_kernel(tc, modulation, h0, c_new, Wo, b_o, Wy, b_y, out):
                         for e in range(2)
                     ],
                 )
-                on_scalar = not (s == 0 and piece in W0_ON_VECTOR)
-                pair_out(on_scalar, gw[s][:].bitcast(F32)[:, (g_ * 2 + u) * 512 : (g_ * 2 + u + 1) * 512], bw)
+                on_scalar = not ((s == 0 and piece in W0_ON_VECTOR) or (s == 1 and piece in W1_ON_VECTOR))
+                pair_out(on_scalar, gw[s][:].bitcast(F32)[:, piece * 512 : (piece + 1) * 512], bw)
 
-        def prep_front(unit):
+        def prep_x(unit):
             bx = act_bank("x", unit)
             hbank[unit] = act_bank("h", unit)
-            bc = act_bank("c", unit)
             gx[unit] = grp3.tile([P, 2048], BF16, tag="gx", name="gx", align_bytes=64)
-            pair_out(True, gx[unit][:].bitcast(F32)[:, 0:512], bx)
+            return bx
+
+        def prep_c(unit, bx):
+            bc = act_bank("c", unit)
+            if bx is not None:
+                pair_out(True, gx[unit][:].bitcast(F32)[:, 0:512], bx)
             t = grp4.tile([P, 1024], F32, tag="tanh", name="tanh")
             nc.scalar.activation(
                 out=t[:].rearrange("p (u e n) -> p u e n", u=2, e=2),
@@ -205,7 +216,7 @@ def tile_flatlstm_pb_t_kernel(tc, modulation, h0, c_new, Wo, b_o, Wy, b_y, out):
                 z = bank("z")
                 for e in range(2):
                     for g_ in range(2):
-                        col = s * 1024 + ((g_ * 2 + u) * 2 + e) * P
+                        col = s * 1024 + ((u * 2 + g_) * 2 + e) * P
                         nc.tensor.matmul_mx(
                             out=z[:, e * CHUNK : (e + 1) * CHUNK],
                             lhsT=wo_codes[:, col : col + P].bitcast(FP8X4),
@@ -280,8 +291,12 @@ def tile_flatlstm_pb_t_kernel(tc, modulation, h0, c_new, Wo, b_o, Wy, b_y, out):
             nc.tensor.transpose(pbo[:, 0:P], zb[:, STREAMS * OUTF : STREAMS * OUTF + 256].bitcast(F32), ident[:])
             nc.vector.tensor_copy(out=bo[:], in_=pbo[:, 0:8].bitcast(BF16))
 
-        load_weights(0)
-        for n in range(PREFETCH):
+        load_weights_wo(0)
+        load_fine("x", 0)
+        load_fine("h", 0)
+        load_fine("c", 0)
+        load_weights_wy(0)
+        for n in range(1, PREFETCH):
             load_unit(n)
         next_load = [PREFETCH]
 
@@ -290,29 +305,35 @@ def tile_flatlstm_pb_t_kernel(tc, modulation, h0, c_new, Wo, b_o, Wy, b_y, out):
         biases()
         weight_piece(0, 2)
         weight_piece(0, 3)
+        bx0 = prep_x(0)
+        pair_out(True, gx[0][:].bitcast(F32)[:, 0:512], bx0)
+        prep_h(0)
+        weight_piece(0, "Q0")
+        weight_piece(0, "Q1")
+        quant_x(0)
+        prep_c(0, None)
         weight_piece(0, "y")
+        weight_piece(0, "QY")
 
         for step in range(-1, UNITS + ADD_LAG):
             a = step + 1
-            if a < UNITS:
-                prep_front(a)
-            if step == -1:
-                weight_piece(0, "Q")
+            fresh = 0 < a < UNITS
+            if fresh:
+                prep_c(a, prep_x(a))
             if 0 <= step - ADD_LAG:
                 add_bias_and_store(step - ADD_LAG)
+            if fresh:
+                prep_h(a)
             if 0 <= step - 1 < UNITS:
                 multiply(step - 1)
-            if a < UNITS:
-                prep_h(a)
-            if step == -1:
-                weight_piece(0, "QY")
-            if 0 <= step - 1 < UNITS:
-                quant_h(step - 1)
-            if a < UNITS:
+            if fresh:
                 quant_x(a)
             if 0 <= step < UNITS - NCHUNK:
-                for piece in W_STEPS[step % NCHUNK]:
+                steps = W_STEPS_FIRST if step < NCHUNK else W_STEPS
+                for piece in steps[step % NCHUNK]:
                     weight_piece(step // NCHUNK + 1, piece)
+            if 0 <= step - 1 < UNITS:
+                quant_h(step - 1)
             if a < UNITS:
                 load_unit(next_load[0])
                 next_load[0] = next_load[0] + 1

@@ -13,46 +13,36 @@ ACT = mybir.ActivationFunctionType
 ALU = mybir.AluOpType
 
 P = 128
-ROWS, STREAMS, FEAT, HID, OUTF = 1024, 4, 512, 512, 256
-CHUNK = 256
-NCHUNK = ROWS // CHUNK
-UNITS = NCHUNK * STREAMS
+ROWS, STREAMS = 1024, 4
+FEAT = 512
+OUTF = 256
+WORDS = FEAT // 2
 BANK = 512
-
-FLOPS = 2 * ROWS * STREAMS * ((FEAT + HID) * HID + HID * OUTF)
-
-PINNED = True
+UNIT_ROWS = 256
+PER_STREAM = ROWS // UNIT_ROWS
+UNITS = STREAMS * PER_STREAM
+WO_BANKS = 4
 PREFETCH = 6
-H_ON_SCALAR = (5, 9, 13)
-W0_ON_VECTOR = (1, 3)
-W1_ON_VECTOR = (2,)
-W_STEPS_FIRST = ((), (), (0, 1, 2), (3, "y", "Q0", "Q1", "QY"))
-W_STEPS = ((0,), (1, "Q0"), (2, "y"), (3, "Q1", "QY"))
-M2_LAG = 2
-ADD_LAG = 3
+
+FLOPS = 2 * ROWS * STREAMS * (2 * FEAT * FEAT + FEAT * OUTF)
 
 
 def tile_flatlstm_pb_t_kernel(tc, modulation, h0, c_new, Wo, b_o, Wy, b_y, out):
     nc = tc.nc
     with ExitStack() as ctx:
         const = ctx.enter_context(tc.tile_pool(name="const", bufs=1))
-        wraw = ctx.enter_context(tc.tile_pool(name="wraw", bufs=2))
-        fine = ctx.enter_context(tc.tile_pool(name="fine", bufs=8))
-        grp2 = ctx.enter_context(tc.tile_pool(name="grp2", bufs=2))
-        grp3 = ctx.enter_context(tc.tile_pool(name="grp3", bufs=3))
-        grp4 = ctx.enter_context(tc.tile_pool(name="grp4", bufs=4))
+        wy_pool = ctx.enter_context(tc.tile_pool(name="wy_pool", bufs=2))
+        work = ctx.enter_context(tc.tile_pool(name="work", bufs=3))
+        slow = ctx.enter_context(tc.tile_pool(name="slow", bufs=4))
+        rows_pool = ctx.enter_context(tc.tile_pool(name="rows_pool", bufs=PREFETCH + 2))
         psum = ctx.enter_context(tc.psum_pool(name="psum", bufs=8))
-        if PINNED:
-            ctx.enter_context(tc.manual_schedule())
+        ctx.enter_context(tc.manual_schedule())
 
-        def bank(label):
-            return psum.tile([P, BANK], F32, tag="bank", name=label)
-
-        zb = const.tile([P, STREAMS * OUTF + 256], BF16, name="zb")
-        nc.vector.memset(zb[:].bitcast(I32), 0)
-        nc.scalar.dma_start(out=zb[0:1, 0 : STREAMS * OUTF], in_=b_y.rearrange("(o s) m -> o (s m)", o=1))
+        bias_rows = const.tile([P, STREAMS * OUTF + 2 * P], BF16, name="bias_rows")
+        nc.vector.memset(bias_rows[:].bitcast(I32), 0)
+        nc.scalar.dma_start(out=bias_rows[0:1, 0 : STREAMS * OUTF], in_=b_y.rearrange("(o s) m -> o (s m)", o=1))
         nc.scalar.dma_start(
-            out=zb[0:8, STREAMS * OUTF : STREAMS * OUTF + 256], in_=b_o.rearrange("s (u q) -> (s u) q", u=2)
+            out=bias_rows[0 : 2 * STREAMS, STREAMS * OUTF :], in_=b_o.rearrange("s (u q) -> (s u) q", u=2)
         )
         warm_in = const.tile([P, 1], F32, name="warm_in")
         warm_out = const.tile([P, 1], F32, name="warm_out")
@@ -63,281 +53,229 @@ def tile_flatlstm_pb_t_kernel(tc, modulation, h0, c_new, Wo, b_o, Wy, b_y, out):
         ones = const.tile([P, P], BF16, name="ones")
         nc.vector.memset(ones[:], 1.0)
 
-        wo_codes = const.tile([P, STREAMS * 1024], U32, name="wo_codes", align_bytes=64)
-        wo_plane = const.tile([P, STREAMS * 1024], U8, name="wo_plane", align_bytes=64)
-        wy_codes = const.tile([P, STREAMS * OUTF], U32, name="wy_codes", align_bytes=64)
-        wy_plane = const.tile([P, STREAMS * OUTF], U8, name="wy_plane", align_bytes=64)
-        by_b = const.tile([P, STREAMS * OUTF], F32, name="by_b")
-        bo = const.tile([P, 16], F32, name="bo")
+        wo_words = const.tile([P, STREAMS * WO_BANKS * 2 * P], U32, name="wo_words", align_bytes=64)
+        wo_scales = const.tile([P, STREAMS * WO_BANKS * 2 * P], U8, name="wo_scales", align_bytes=64)
+        wy_words = const.tile([P, STREAMS * OUTF], U32, name="wy_words", align_bytes=64)
+        wy_scales = const.tile([P, STREAMS * OUTF], U8, name="wy_scales", align_bytes=64)
+        by_all = const.tile([P, STREAMS * OUTF], F32, name="by_all")
+        bo_cols = const.tile([P, 4 * STREAMS], F32, name="bo_cols")
 
-        raw = {}
+        sources = {"x": modulation, "h": h0, "c": c_new}
+        rows = {}
         wo_raw = {}
         wy_raw = {}
-        srcs = {"x": modulation, "h": h0, "c": c_new}
+        h_bank, xh_grouped, xh_mx, tanh_c, gate, h_grouped, h_mx, y_bank, w_grouped = {}, {}, {}, {}, {}, {}, {}, {}, {}
 
-        def load_fine(kind, unit):
-            s, k = unit // NCHUNK, unit % NCHUNK
-            t = fine.tile([P, 2 * FEAT], BF16, tag="fine_" + kind, name="fine_" + kind)
+        def load_rows(kind, unit):
+            s, r0 = unit // PER_STREAM, (unit % PER_STREAM) * UNIT_ROWS
+            t = rows_pool.tile([P, 2 * FEAT], BF16, tag="rows_" + kind, name="rows_" + kind)
             nc.sync.dma_start(
                 out=t[:].rearrange("p (j d) -> p j d", j=2),
-                in_=srcs[kind][k * CHUNK : (k + 1) * CHUNK, s * FEAT : (s + 1) * FEAT].rearrange(
-                    "(p j) d -> p j d", j=2
-                ),
+                in_=sources[kind][r0 : r0 + UNIT_ROWS, s * FEAT : (s + 1) * FEAT].rearrange("(p j) d -> p j d", j=2),
             )
-            raw[(kind, unit)] = t[:].bitcast(F32)
+            rows[(kind, unit)] = t[:].bitcast(F32)
 
-        def load_weights_wo(s):
-            t = wraw.tile([P, 4096], BF16, tag="wo_raw", name="wo_raw")
-            for u in range(2):
-                nc.sync.dma_start(
-                    out=t[:, u * 2048 : (u + 1) * 2048],
-                    in_=Wo[s][u * 256 : (u + 1) * 256, :].rearrange("(p e) d -> p (e d)", e=2),
-                )
-            wo_raw[s] = t[:].bitcast(F32)
+        def load_wo_half(s, u):
+            t = slow.tile([P, 4 * FEAT], BF16, tag="wo_raw", name="wo_raw")
+            nc.sync.dma_start(out=t[:], in_=Wo[s][u * 2 * P : (u + 1) * 2 * P, :].rearrange("(p e) d -> p (e d)", e=2))
+            wo_raw[(s, u)] = t[:].bitcast(F32)
 
-        def load_weights_wy(s):
-            t2 = wraw.tile([P, 1024], BF16, tag="wy_raw", name="wy_raw")
-            nc.sync.dma_start(out=t2[:], in_=Wy[s].rearrange("(pm jm) l -> pm (jm l)", jm=2))
-            wy_raw[s] = t2[:].bitcast(F32)
+        def load_wy(s):
+            t = wy_pool.tile([P, 2 * FEAT], BF16, tag="wy_raw", name="wy_raw")
+            nc.sync.dma_start(
+                out=t[:].rearrange("p (j l) -> p j l", j=2), in_=Wy[s].rearrange("(j p) l -> p j l", j=2)
+            )
+            wy_raw[s] = t[:].bitcast(F32)
 
-        def load_unit(n):
-            if n >= UNITS:
+        def load_for_unit(unit):
+            if unit >= UNITS:
                 return
-            if n % NCHUNK == NCHUNK - 1 and n // NCHUNK + 1 < STREAMS:
-                load_weights_wo(n // NCHUNK + 1)
-                load_weights_wy(n // NCHUNK + 1)
-            load_fine("x", n)
-            load_fine("h", n)
-            load_fine("c", n)
+            following, k = unit // PER_STREAM + 1, unit % PER_STREAM
+            if following < STREAMS:
+                if k == 1:
+                    load_wo_half(following, 0)
+                elif k == 2:
+                    load_wy(following)
+                elif k == 3:
+                    load_wo_half(following, 1)
+            for kind in ("x", "h", "c"):
+                load_rows(kind, unit)
 
-        def transpose4(dst, views):
-            for q, v in enumerate(views):
-                nc.tensor.transpose(dst[:, q * P : (q + 1) * P], v, ident[:])
+        def transposed_bank(words, base, row_step):
+            bank = psum.tile([P, BANK], F32, tag="bank", name="bank")
+            for u in range(2):
+                for j in range(2):
+                    lo = base + j * row_step + u * P
+                    q = 2 * u + j
+                    nc.tensor.transpose(bank[:, q * P : (q + 1) * P], words[:, lo : lo + P], ident[:])
+            return bank
 
-        def pair_out(on_scalar, dst_words, src):
-            o = dst_words.rearrange("p (n u) -> p n u", u=2)
-            i = src[:].rearrange("p (u n) -> p n u", u=2)
-            if on_scalar:
-                nc.scalar.copy(out=o, in_=i)
+        def copy_grouped(engine, grouped_words, bank):
+            dst = grouped_words.rearrange("p (n u) -> p n u", u=2)
+            src = bank[:].rearrange("p (u n) -> p n u", u=2)
+            if engine == "scalar":
+                nc.scalar.copy(out=dst, in_=src)
             else:
-                nc.vector.tensor_copy(out=o, in_=i)
+                nc.vector.tensor_copy(out=dst, in_=src)
 
-        def act_bank(kind, unit):
-            w = raw[(kind, unit)]
-            b = bank("b" + kind)
-            transpose4(b, [w[:, j * 256 + u * P : j * 256 + (u + 1) * P] for u in range(2) for j in range(2)])
-            return b
+        def quantise(grouped, words, scales):
+            nc.vector.quantize_mx(out=words.bitcast(FP8X4), scales=scales, in_=grouped)
 
-        gx = {}
-        gw = {}
-        gwy = {}
-        xc = {}
-        tanh_c = {}
-        hcodes = {}
-        gate = {}
-        hgs = {}
-        ybank = {}
-        hbank = {}
+        def weight_bank(key, words, base, row_step):
+            bank = transposed_bank(words, base, row_step)
+            w_grouped[key] = work.tile([P, 4 * 2 * P], BF16, tag="w_grouped", name="w_grouped", align_bytes=64)
+            copy_grouped("scalar", w_grouped[key][:].bitcast(F32), bank)
 
-        def weight_piece(s, piece):
-            if piece == "y":
-                wyw = wy_raw[s]
-                by = bank("bwy")
-                transpose4(by, [wyw[:, jm * 256 + u * P : jm * 256 + (u + 1) * P] for u in range(2) for jm in range(2)])
-                gyt = grp2.tile([P, 1024], BF16, tag="gwy", name="gwy", align_bytes=64)
-                nc.vector.tensor_copy(
-                    out=gyt[:].bitcast(F32).rearrange("p (pm jm u) -> p pm jm u", jm=2, u=2),
-                    in_=by[:].rearrange("p (u jm pm) -> p pm jm u", u=2, jm=2),
-                )
-                gwy[s] = gyt
-            elif piece == "Q0" or piece == "Q1":
-                u = 0 if piece == "Q0" else 1
-                lo = s * 1024 + u * 512
-                nc.vector.quantize_mx(
-                    out=wo_codes[:, lo : lo + 512].bitcast(FP8X4),
-                    scales=wo_plane[:, lo : lo + 512],
-                    in_=gw[s][:, u * 2048 : (u + 1) * 2048],
-                )
-            elif piece == "QY":
-                nc.vector.quantize_mx(
-                    out=wy_codes[:, s * OUTF : (s + 1) * OUTF].bitcast(FP8X4),
-                    scales=wy_plane[:, s * OUTF : (s + 1) * OUTF],
-                    in_=gwy[s][:],
-                )
-            else:
-                u, g_ = piece // 2, piece % 2
-                if piece == 0:
-                    gw[s] = grp2.tile([P, 4096], BF16, tag="gw", name="gw", align_bytes=64)
-                ww = wo_raw[s]
-                bw = bank("bw")
-                transpose4(
-                    bw,
-                    [
-                        ww[:, u * 1024 + e * 512 + g_ * 256 + u2 * P : u * 1024 + e * 512 + g_ * 256 + (u2 + 1) * P]
-                        for u2 in range(2)
-                        for e in range(2)
-                    ],
-                )
-                on_scalar = not ((s == 0 and piece in W0_ON_VECTOR) or (s == 1 and piece in W1_ON_VECTOR))
-                pair_out(on_scalar, gw[s][:].bitcast(F32)[:, piece * 512 : (piece + 1) * 512], bw)
+        def wo_start(s, b):
+            return (s * WO_BANKS + b) * 2 * P
 
-        def prep_x(unit):
-            bx = act_bank("x", unit)
-            hbank[unit] = act_bank("h", unit)
-            gx[unit] = grp3.tile([P, 2048], BF16, tag="gx", name="gx", align_bytes=64)
-            return bx
+        def stream_columns(s):
+            return slice(s * OUTF, (s + 1) * OUTF)
 
-        def prep_c(unit, bx):
-            bc = act_bank("c", unit)
-            if bx is not None:
-                pair_out(True, gx[unit][:].bitcast(F32)[:, 0:512], bx)
-            t = grp4.tile([P, 1024], F32, tag="tanh", name="tanh")
+        def weights_step(s, k):
+            weight_bank(("wo", s, k), wo_raw[(s, k // 2)], (k % 2) * WORDS, 2 * WORDS)
+            if k == 2:
+                weight_bank(("wy", s), wy_raw[s], 0, WORDS)
+
+        def weights_quantise(s, k):
+            cols = slice(wo_start(s, k), wo_start(s, k) + 2 * P)
+            quantise(w_grouped[("wo", s, k)][:], wo_words[:, cols], wo_scales[:, cols])
+            if k == 3:
+                cols = stream_columns(s)
+                quantise(w_grouped[("wy", s)][:], wy_words[:, cols], wy_scales[:, cols])
+
+        def biases():
+            for half in range(2):
+                spread = psum.tile([P, BANK], F32, tag="bank", name="spread")
+                cols = slice(half * BANK, (half + 1) * BANK)
+                nc.tensor.matmul(out=spread[:], lhsT=ones[:], rhs=bias_rows[:, cols], start=True, stop=True)
+                nc.vector.tensor_copy(out=by_all[:, cols], in_=spread[:])
+            turned = psum.tile([P, BANK], F32, tag="bank", name="turned")
+            nc.tensor.transpose(turned[:, 0:P], bias_rows[:, STREAMS * OUTF :].bitcast(F32), ident[:])
+            nc.vector.tensor_copy(out=bo_cols[:], in_=turned[:, 0 : 2 * STREAMS].bitcast(BF16))
+
+        def unit_front(unit):
+            x_bank = transposed_bank(rows[("x", unit)], 0, WORDS)
+            h_bank[unit] = transposed_bank(rows[("h", unit)], 0, WORDS)
+            c_bank = transposed_bank(rows[("c", unit)], 0, WORDS)
+            xh_grouped[unit] = work.tile([P, 2 * 4 * UNIT_ROWS], BF16, tag="xh_grouped", name="xh_grouped", align_bytes=64)
+            copy_grouped("scalar", xh_grouped[unit][:].bitcast(F32)[:, 0:BANK], x_bank)
+            tanh_c[unit] = slow.tile([P, 4 * UNIT_ROWS], F32, tag="tanh_c", name="tanh_c")
             nc.scalar.activation(
-                out=t[:].rearrange("p (u e n) -> p u e n", u=2, e=2),
-                in_=bc[:].bitcast(BF16).rearrange("p (u n e) -> p u e n", u=2, e=2),
+                out=tanh_c[unit][:].rearrange("p (u e n) -> p u e n", u=2, e=2),
+                in_=c_bank[:].bitcast(BF16).rearrange("p (u n e) -> p u e n", u=2, e=2),
                 func=ACT.Tanh,
             )
-            tanh_c[unit] = t
 
-        def prep_h(unit):
-            pair_out(unit in H_ON_SCALAR, gx[unit][:].bitcast(F32)[:, 512:1024], hbank[unit])
+        def copy_h(unit):
+            copy_grouped("vector", xh_grouped[unit][:].bitcast(F32)[:, BANK : 2 * BANK], h_bank[unit])
 
-        def quant_x(unit):
-            codes = grp3.tile([P, 512], U32, tag="xc", name="xc", align_bytes=64)
-            plane = grp3.tile([P, 512], U8, tag="xp", name="xp", align_bytes=64)
-            nc.vector.quantize_mx(out=codes[:].bitcast(FP8X4), scales=plane[:], in_=gx[unit][:])
-            xc[unit] = (codes, plane)
+        def quantise_xh(unit):
+            words = work.tile([P, 2 * UNIT_ROWS], U32, tag="xh_words", name="xh_words", align_bytes=64)
+            scales = work.tile([P, 2 * UNIT_ROWS], U8, tag="xh_scales", name="xh_scales", align_bytes=64)
+            quantise(xh_grouped[unit][:], words[:], scales[:])
+            xh_mx[unit] = (words, scales)
 
-        def stage1(unit):
-            s = unit // NCHUNK
-            codes, plane = xc[unit]
-            o = grp3.tile([P, 1024], F32, tag="gate", name="gate")
+        def gate_of(unit):
+            s = unit // PER_STREAM
+            words, scales = xh_mx[unit]
+            gate[unit] = work.tile([P, 4 * UNIT_ROWS], F32, tag="gate", name="gate")
             for u in range(2):
-                z = bank("z")
+                z = psum.tile([P, BANK], F32, tag="bank", name="z")
                 for e in range(2):
-                    for g_ in range(2):
-                        col = s * 1024 + ((u * 2 + g_) * 2 + e) * P
+                    for g in range(2):
+                        lo = wo_start(s, 2 * u + g) + e * P
                         nc.tensor.matmul_mx(
-                            out=z[:, e * CHUNK : (e + 1) * CHUNK],
-                            lhsT=wo_codes[:, col : col + P].bitcast(FP8X4),
-                            lhsT_scale=wo_plane[:, col : col + P],
-                            rhs=codes[:, g_ * CHUNK : (g_ + 1) * CHUNK].bitcast(FP8X4),
-                            rhs_scale=plane[:, g_ * CHUNK : (g_ + 1) * CHUNK],
-                            start=(g_ == 0),
-                            stop=(g_ == 1),
+                            out=z[:, e * UNIT_ROWS : (e + 1) * UNIT_ROWS],
+                            lhsT=wo_words[:, lo : lo + P].bitcast(FP8X4),
+                            lhsT_scale=wo_scales[:, lo : lo + P],
+                            rhs=words[:, g * UNIT_ROWS : (g + 1) * UNIT_ROWS].bitcast(FP8X4),
+                            rhs_scale=scales[:, g * UNIT_ROWS : (g + 1) * UNIT_ROWS],
+                            start=(g == 0),
+                            stop=(g == 1),
                         )
                 for e in range(2):
-                    tt = u * 2 + e
+                    t = 2 * u + e
                     nc.scalar.activation(
-                        out=o[:, tt * CHUNK : (tt + 1) * CHUNK],
-                        in_=z[:, e * CHUNK : (e + 1) * CHUNK],
+                        out=gate[unit][:, t * UNIT_ROWS : (t + 1) * UNIT_ROWS],
+                        in_=z[:, e * UNIT_ROWS : (e + 1) * UNIT_ROWS],
                         func=ACT.Sigmoid,
-                        bias=bo[:, s * 4 + tt : s * 4 + tt + 1],
+                        bias=bo_cols[:, 4 * s + t : 4 * s + t + 1],
                     )
-            gate[unit] = o
 
-        def multiply(unit):
-            hg = grp3.tile([P, 1024], BF16, tag="hg", name="hg", align_bytes=64)
+        def gating_product(unit):
+            h_grouped[unit] = work.tile([P, 4 * UNIT_ROWS], BF16, tag="h_grouped", name="h_grouped", align_bytes=64)
             nc.vector.tensor_tensor(
-                out=hg[:].rearrange("p (c i t) -> p c t i", i=4, t=4),
+                out=h_grouped[unit][:].rearrange("p (c i t) -> p c t i", i=4, t=4),
                 in0=gate[unit][:].rearrange("p (t c i) -> p c t i", t=4, i=4),
                 in1=tanh_c[unit][:].rearrange("p (t c i) -> p c t i", t=4, i=4),
                 op=ALU.mult,
             )
-            hgs[unit] = hg
 
-        def quant_h(unit):
-            codes = grp3.tile([P, CHUNK], U32, tag="hc", name="hc", align_bytes=64)
-            plane = grp3.tile([P, CHUNK], U8, tag="hp", name="hp", align_bytes=64)
-            nc.vector.quantize_mx(out=codes[:].bitcast(FP8X4), scales=plane[:], in_=hgs[unit][:])
-            hcodes[unit] = (codes, plane)
+        def quantise_h(unit):
+            words = work.tile([P, UNIT_ROWS], U32, tag="h_words", name="h_words", align_bytes=64)
+            scales = work.tile([P, UNIT_ROWS], U8, tag="h_scales", name="h_scales", align_bytes=64)
+            quantise(h_grouped[unit][:], words[:], scales[:])
+            h_mx[unit] = (words, scales)
 
-        def stage2(unit):
-            s = unit // NCHUNK
-            codes, plane = hcodes[unit]
-            y = bank("y")
+        def projection(unit):
+            cols = stream_columns(unit // PER_STREAM)
+            words, scales = h_mx[unit]
+            y_bank[unit] = psum.tile([P, BANK], F32, tag="bank", name="y")
             for j in range(2):
                 nc.tensor.matmul_mx(
-                    out=y[:, j * OUTF : (j + 1) * OUTF],
-                    lhsT=codes[:, j * P : (j + 1) * P].bitcast(FP8X4),
-                    lhsT_scale=plane[:, j * P : (j + 1) * P],
-                    rhs=wy_codes[:, s * OUTF : (s + 1) * OUTF].bitcast(FP8X4),
-                    rhs_scale=wy_plane[:, s * OUTF : (s + 1) * OUTF],
+                    out=y_bank[unit][:, j * OUTF : (j + 1) * OUTF],
+                    lhsT=words[:, j * P : (j + 1) * P].bitcast(FP8X4),
+                    lhsT_scale=scales[:, j * P : (j + 1) * P],
+                    rhs=wy_words[:, cols].bitcast(FP8X4),
+                    rhs_scale=wy_scales[:, cols],
                     start=True,
                     stop=True,
                 )
-            ybank[unit] = y
 
         def add_bias_and_store(unit):
-            s, k = unit // NCHUNK, unit % NCHUNK
-            res = grp4.tile([P, 2 * OUTF], F32, tag="res", name="res")
+            cols, r0 = stream_columns(unit // PER_STREAM), (unit % PER_STREAM) * UNIT_ROWS
+            y = slow.tile([P, 2 * OUTF], F32, tag="y_sb", name="y_sb")
             nc.vector.tensor_tensor(
-                out=res[:].rearrange("p (j m) -> p j m", j=2),
-                in0=ybank[unit][:].rearrange("p (j m) -> p j m", j=2),
-                in1=by_b[:, s * OUTF : (s + 1) * OUTF].unsqueeze(1).to_broadcast([P, 2, OUTF]),
+                out=y[:].rearrange("p (j m) -> p j m", j=2),
+                in0=y_bank[unit][:].rearrange("p (j m) -> p j m", j=2),
+                in1=by_all[:, cols].unsqueeze(1).to_broadcast([P, 2, OUTF]),
                 op=ALU.add,
             )
             nc.sync.dma_start(
-                out=out[k * CHUNK : (k + 1) * CHUNK, s * OUTF : (s + 1) * OUTF].rearrange("(p j) m -> p j m", j=2),
-                in_=res[:].rearrange("p (j m) -> p j m", j=2),
+                out=out[r0 : r0 + UNIT_ROWS, cols].rearrange("(p j) m -> p j m", j=2),
+                in_=y[:].rearrange("p (j m) -> p j m", j=2),
             )
 
-        def biases():
-            for c in range(2):
-                pb = bank("pb")
-                nc.tensor.matmul(out=pb[:], lhsT=ones[:], rhs=zb[:, c * BANK : (c + 1) * BANK], start=True, stop=True)
-                nc.vector.tensor_copy(out=by_b[:, c * BANK : (c + 1) * BANK], in_=pb[:])
-            pbo = bank("pbo")
-            nc.tensor.transpose(pbo[:, 0:P], zb[:, STREAMS * OUTF : STREAMS * OUTF + 256].bitcast(F32), ident[:])
-            nc.vector.tensor_copy(out=bo[:], in_=pbo[:, 0:8].bitcast(BF16))
+        load_wo_half(0, 0)
+        load_wo_half(0, 1)
+        load_wy(0)
+        for unit in range(PREFETCH):
+            load_for_unit(unit)
 
-        load_weights_wo(0)
-        load_fine("x", 0)
-        load_fine("h", 0)
-        load_fine("c", 0)
-        load_weights_wy(0)
-        for n in range(1, PREFETCH):
-            load_unit(n)
-        next_load = [PREFETCH]
-
-        weight_piece(0, 0)
-        weight_piece(0, 1)
-        biases()
-        weight_piece(0, 2)
-        weight_piece(0, 3)
-        bx0 = prep_x(0)
-        pair_out(True, gx[0][:].bitcast(F32)[:, 0:512], bx0)
-        prep_h(0)
-        weight_piece(0, "Q0")
-        weight_piece(0, "Q1")
-        quant_x(0)
-        prep_c(0, None)
-        weight_piece(0, "y")
-        weight_piece(0, "QY")
-
-        for step in range(-1, UNITS + ADD_LAG):
-            a = step + 1
-            fresh = 0 < a < UNITS
-            if fresh:
-                prep_c(a, prep_x(a))
-            if 0 <= step - ADD_LAG:
-                add_bias_and_store(step - ADD_LAG)
-            if fresh:
-                prep_h(a)
+        for step in range(-PER_STREAM, UNITS + 3):
+            following, k = step // PER_STREAM + 1, step % PER_STREAM
+            if following < STREAMS:
+                weights_step(following, k)
+            if 0 <= step + 1 < UNITS:
+                unit_front(step + 1)
+            if step == -2:
+                biases()
+            if 0 <= step - 3:
+                add_bias_and_store(step - 3)
+            if 0 <= step + 1 < UNITS:
+                copy_h(step + 1)
             if 0 <= step - 1 < UNITS:
-                multiply(step - 1)
-            if fresh:
-                quant_x(a)
-            if 0 <= step < UNITS - NCHUNK:
-                steps = W_STEPS_FIRST if step < NCHUNK else W_STEPS
-                for piece in steps[step % NCHUNK]:
-                    weight_piece(step // NCHUNK + 1, piece)
+                gating_product(step - 1)
+            if 0 <= step + 1 < UNITS:
+                quantise_xh(step + 1)
             if 0 <= step - 1 < UNITS:
-                quant_h(step - 1)
-            if a < UNITS:
-                load_unit(next_load[0])
-                next_load[0] = next_load[0] + 1
+                quantise_h(step - 1)
+            if following < STREAMS:
+                weights_quantise(following, k)
+            if 0 <= step + 1:
+                load_for_unit(step + 1 + PREFETCH)
             if 0 <= step < UNITS:
-                stage1(step)
-            if 0 <= step - M2_LAG < UNITS:
-                stage2(step - M2_LAG)
+                gate_of(step)
+            if 0 <= step - 2 < UNITS:
+                projection(step - 2)

@@ -36,7 +36,6 @@ def tile_flatlstm_pb_t_kernel(tc, modulation, h0, c_new, Wo, b_o, Wy, b_y, out):
         slow = ctx.enter_context(tc.tile_pool(name="slow", bufs=4))
         rows_pool = ctx.enter_context(tc.tile_pool(name="rows_pool", bufs=PREFETCH + 2))
         psum = ctx.enter_context(tc.psum_pool(name="psum", bufs=8))
-        ctx.enter_context(tc.manual_schedule())
 
         bias_rows = const.tile([P, STREAMS * OUTF + 2 * P], BF16, name="bias_rows")
         nc.vector.memset(bias_rows[:].bitcast(I32), 0)

@@ -36,6 +36,7 @@ def tile_flatlstm_pb_t_kernel(tc, modulation, h0, c_new, Wo, b_o, Wy, b_y, out):
         slow = ctx.enter_context(tc.tile_pool(name="slow", bufs=4))
         rows_pool = ctx.enter_context(tc.tile_pool(name="rows_pool", bufs=PREFETCH + 2))
         psum = ctx.enter_context(tc.psum_pool(name="psum", bufs=8))
+        ctx.enter_context(tc.manual_schedule())
 
         bias_rows = const.tile([P, STREAMS * OUTF + 2 * P], BF16, name="bias_rows")
         nc.vector.memset(bias_rows[:].bitcast(I32), 0)
@@ -89,16 +90,13 @@ def tile_flatlstm_pb_t_kernel(tc, modulation, h0, c_new, Wo, b_o, Wy, b_y, out):
         def load_for_unit(unit):
             if unit >= UNITS:
                 return
-            following, k = unit // PER_STREAM + 1, unit % PER_STREAM
-            if following < STREAMS:
-                if k == 1:
-                    load_wo_half(following, 0)
-                elif k == 2:
-                    load_wy(following)
-                elif k == 3:
-                    load_wo_half(following, 1)
+            s, k = unit // PER_STREAM, unit % PER_STREAM
+            if s + 1 < STREAMS and k % 2 == 1:
+                load_wo_half(s + 1, k // 2)
             for kind in ("x", "h", "c"):
                 load_rows(kind, unit)
+            if k == 0:
+                load_wy(s)
 
         def transposed_bank(words, base, row_step):
             bank = psum.tile([P, BANK], F32, tag="bank", name="bank")
@@ -131,10 +129,11 @@ def tile_flatlstm_pb_t_kernel(tc, modulation, h0, c_new, Wo, b_o, Wy, b_y, out):
         def stream_columns(s):
             return slice(s * OUTF, (s + 1) * OUTF)
 
-        def weights_step(s, k):
+        def wo_bank(s, k):
             weight_bank(("wo", s, k), wo_raw[(s, k // 2)], (k % 2) * WORDS, 2 * WORDS)
-            if k == 2:
-                weight_bank(("wy", s), wy_raw[s], 0, WORDS)
+
+        def wy_bank(s):
+            weight_bank(("wy", s), wy_raw[s], 0, WORDS)
 
         def weights_quantise(s, k):
             cols = slice(wo_start(s, k), wo_start(s, k) + 2 * P)
@@ -248,16 +247,19 @@ def tile_flatlstm_pb_t_kernel(tc, modulation, h0, c_new, Wo, b_o, Wy, b_y, out):
 
         load_wo_half(0, 0)
         load_wo_half(0, 1)
-        load_wy(0)
         for unit in range(PREFETCH):
             load_for_unit(unit)
 
         for step in range(-PER_STREAM, UNITS + 3):
             following, k = step // PER_STREAM + 1, step % PER_STREAM
+            if step == 0:
+                gate_of(0)
             if following < STREAMS:
-                weights_step(following, k)
+                wo_bank(following, k)
             if 0 <= step + 1 < UNITS:
                 unit_front(step + 1)
+            if following < STREAMS and k == PER_STREAM - 1:
+                wy_bank(following)
             if step == -2:
                 biases()
             if 0 <= step - 3:
@@ -274,7 +276,7 @@ def tile_flatlstm_pb_t_kernel(tc, modulation, h0, c_new, Wo, b_o, Wy, b_y, out):
                 weights_quantise(following, k)
             if 0 <= step + 1:
                 load_for_unit(step + 1 + PREFETCH)
-            if 0 <= step < UNITS:
+            if 0 < step < UNITS:
                 gate_of(step)
             if 0 <= step - 2 < UNITS:
                 projection(step - 2)

@@ -21,8 +21,12 @@ BANK = 512
 UNIT_ROWS = 256
 PER_STREAM = ROWS // UNIT_ROWS
 UNITS = STREAMS * PER_STREAM
+LAST = UNITS - 1
 WO_BANKS = 4
 PREFETCH = 6
+
+XH, HN, WB = 0, 4 * BANK, 6 * BANK
+BATCH = 8 * BANK
 
 FLOPS = 2 * ROWS * STREAMS * (2 * FEAT * FEAT + FEAT * OUTF)
 
@@ -31,11 +35,15 @@ def tile_flatlstm_pb_t_kernel(tc, modulation, h0, c_new, Wo, b_o, Wy, b_y, out):
     nc = tc.nc
     with ExitStack() as ctx:
         const = ctx.enter_context(tc.tile_pool(name="const", bufs=1))
+        wo_pool = ctx.enter_context(tc.tile_pool(name="wo_pool", bufs=6))
         wy_pool = ctx.enter_context(tc.tile_pool(name="wy_pool", bufs=2))
         work = ctx.enter_context(tc.tile_pool(name="work", bufs=3))
         slow = ctx.enter_context(tc.tile_pool(name="slow", bufs=4))
+        mx_pool = ctx.enter_context(tc.tile_pool(name="mx_pool", bufs=9))
         rows_pool = ctx.enter_context(tc.tile_pool(name="rows_pool", bufs=PREFETCH + 2))
-        psum = ctx.enter_context(tc.psum_pool(name="psum", bufs=8))
+        psum_t = ctx.enter_context(tc.psum_pool(name="psum_t", bufs=4))
+        psum_z = ctx.enter_context(tc.psum_pool(name="psum_z", bufs=2))
+        psum_y = ctx.enter_context(tc.psum_pool(name="psum_y", bufs=2))
         ctx.enter_context(tc.manual_schedule())
 
         bias_rows = const.tile([P, STREAMS * OUTF + 2 * P], BF16, name="bias_rows")
@@ -53,8 +61,6 @@ def tile_flatlstm_pb_t_kernel(tc, modulation, h0, c_new, Wo, b_o, Wy, b_y, out):
         ones = const.tile([P, P], BF16, name="ones")
         nc.vector.memset(ones[:], 1.0)
 
-        wo_words = const.tile([P, STREAMS * WO_BANKS * 2 * P], U32, name="wo_words", align_bytes=64)
-        wo_scales = const.tile([P, STREAMS * WO_BANKS * 2 * P], U8, name="wo_scales", align_bytes=64)
         wy_words = const.tile([P, STREAMS * OUTF], U32, name="wy_words", align_bytes=64)
         wy_scales = const.tile([P, STREAMS * OUTF], U8, name="wy_scales", align_bytes=64)
         by_all = const.tile([P, STREAMS * OUTF], F32, name="by_all")
@@ -64,7 +70,10 @@ def tile_flatlstm_pb_t_kernel(tc, modulation, h0, c_new, Wo, b_o, Wy, b_y, out):
         rows = {}
         wo_raw = {}
         wy_raw = {}
-        h_bank, xh_grouped, xh_mx, tanh_c, gate, h_grouped, h_mx, y_bank, w_grouped = {}, {}, {}, {}, {}, {}, {}, {}, {}
+        grouped = {}
+        mx = {}
+        wo_mx = {}
+        wy_grouped, tanh_c, gate, y_bank, turned_bank = {}, {}, {}, {}, {}
 
         def load_rows(kind, unit):
             s, r0 = unit // PER_STREAM, (unit % PER_STREAM) * UNIT_ROWS
@@ -76,7 +85,7 @@ def tile_flatlstm_pb_t_kernel(tc, modulation, h0, c_new, Wo, b_o, Wy, b_y, out):
             rows[(kind, unit)] = t[:].bitcast(F32)
 
         def load_wo_half(s, u):
-            t = slow.tile([P, 4 * FEAT], BF16, tag="wo_raw", name="wo_raw")
+            t = wo_pool.tile([P, 4 * FEAT], BF16, tag="wo_raw", name="wo_raw")
             nc.sync.dma_start(out=t[:], in_=Wo[s][u * 2 * P : (u + 1) * 2 * P, :].rearrange("(p e) d -> p (e d)", e=2))
             wo_raw[(s, u)] = t[:].bitcast(F32)
 
@@ -91,192 +100,269 @@ def tile_flatlstm_pb_t_kernel(tc, modulation, h0, c_new, Wo, b_o, Wy, b_y, out):
             if unit >= UNITS:
                 return
             s, k = unit // PER_STREAM, unit % PER_STREAM
-            if s + 1 < STREAMS and k % 2 == 1:
-                load_wo_half(s + 1, k // 2)
             for kind in ("x", "h", "c"):
                 load_rows(kind, unit)
-            if k == 0:
+            if s + 1 < STREAMS and k % 2 == 1:
+                load_wo_half(s + 1, k // 2)
+            if k == 1:
                 load_wy(s)
 
-        def transposed_bank(words, base, row_step):
-            bank = psum.tile([P, BANK], F32, tag="bank", name="bank")
+        def batch_of(j):
+            if j not in grouped:
+                grouped[j] = work.tile([P, BATCH], BF16, tag="grouped", name="grouped", align_bytes=64)
+            return grouped[j]
+
+        def turn(key, words, base, row_step):
+            bank = psum_t.tile([P, BANK], F32, tag="turned", name="turned")
             for u in range(2):
                 for j in range(2):
                     lo = base + j * row_step + u * P
                     q = 2 * u + j
                     nc.tensor.transpose(bank[:, q * P : (q + 1) * P], words[:, lo : lo + P], ident[:])
-            return bank
+            turned_bank[key] = bank
 
-        def copy_grouped(engine, grouped_words, bank):
+        def copy_grouped(engine, key, grouped_words):
             dst = grouped_words.rearrange("p (n u) -> p n u", u=2)
-            src = bank[:].rearrange("p (u n) -> p n u", u=2)
+            src = turned_bank[key][:].rearrange("p (u n) -> p n u", u=2)
             if engine == "scalar":
                 nc.scalar.copy(out=dst, in_=src)
             else:
                 nc.vector.tensor_copy(out=dst, in_=src)
 
-        def quantise(grouped, words, scales):
-            nc.vector.quantize_mx(out=words.bitcast(FP8X4), scales=scales, in_=grouped)
+        def turn_rows(kind, unit):
+            turn((kind, unit), rows[(kind, unit)], 0, WORDS)
 
-        def weight_bank(key, words, base, row_step):
-            bank = transposed_bank(words, base, row_step)
-            w_grouped[key] = work.tile([P, 4 * 2 * P], BF16, tag="w_grouped", name="w_grouped", align_bytes=64)
-            copy_grouped("scalar", w_grouped[key][:].bitcast(F32), bank)
+        def turn_wo(s, b):
+            turn(("wo", s, b), wo_raw[(s, b // 2)], (b % 2) * WORDS, 2 * WORDS)
 
-        def wo_start(s, b):
-            return (s * WO_BANKS + b) * 2 * P
+        def copy_rows(engine, kind, unit):
+            lo = XH + (0 if kind == "x" else 2 * BANK)
+            copy_grouped(engine, (kind, unit), batch_of(unit)[:, lo : lo + 2 * BANK].bitcast(F32))
+
+        def copy_wo(engine, s, b, j):
+            copy_grouped(engine, ("wo", s, b), batch_of(j)[:, WB : WB + 2 * BANK].bitcast(F32))
+
+        def copy_wy(engine, s):
+            wy_grouped[s] = wy_pool.tile([P, 2 * BANK], BF16, tag="wy_grouped", name="wy_grouped", align_bytes=64)
+            copy_grouped(engine, ("wy", s), wy_grouped[s][:].bitcast(F32))
+
+        def quantise(words, scales, values):
+            nc.vector.quantize_mx(out=words.bitcast(FP8X4), scales=scales, in_=values)
+
+        def quantise_batch(j, lo, hi):
+            if j not in mx:
+                words = mx_pool.tile([P, BATCH // 4], U32, tag="mx_words", name="mx_words", align_bytes=64)
+                scales = mx_pool.tile([P, BATCH // 4], U8, tag="mx_scales", name="mx_scales", align_bytes=64)
+                mx[j] = (words, scales)
+            words, scales = mx[j]
+            quantise(words[:, lo // 4 : hi // 4], scales[:, lo // 4 : hi // 4], grouped[j][:, lo:hi])
+
+        def keep_wo(s, b, j):
+            cols = slice(WB // 4, BATCH // 4)
+            wo_mx[(s, b)] = (mx[j][0][:, cols], mx[j][1][:, cols])
 
         def stream_columns(s):
             return slice(s * OUTF, (s + 1) * OUTF)
 
-        def wo_bank(s, k):
-            weight_bank(("wo", s, k), wo_raw[(s, k // 2)], (k % 2) * WORDS, 2 * WORDS)
+        def quantise_wy(s):
+            cols = stream_columns(s)
+            quantise(wy_words[:, cols], wy_scales[:, cols], wy_grouped[s][:])
 
-        def wy_bank(s):
-            weight_bank(("wy", s), wy_raw[s], 0, WORDS)
-
-        def weights_quantise(s, k):
-            cols = slice(wo_start(s, k), wo_start(s, k) + 2 * P)
-            quantise(w_grouped[("wo", s, k)][:], wo_words[:, cols], wo_scales[:, cols])
-            if k == 3:
-                cols = stream_columns(s)
-                quantise(w_grouped[("wy", s)][:], wy_words[:, cols], wy_scales[:, cols])
-
-        def biases():
-            for half in range(2):
-                spread = psum.tile([P, BANK], F32, tag="bank", name="spread")
-                cols = slice(half * BANK, (half + 1) * BANK)
-                nc.tensor.matmul(out=spread[:], lhsT=ones[:], rhs=bias_rows[:, cols], start=True, stop=True)
-                nc.vector.tensor_copy(out=by_all[:, cols], in_=spread[:])
-            turned = psum.tile([P, BANK], F32, tag="bank", name="turned")
-            nc.tensor.transpose(turned[:, 0:P], bias_rows[:, STREAMS * OUTF :].bitcast(F32), ident[:])
-            nc.vector.tensor_copy(out=bo_cols[:], in_=turned[:, 0 : 2 * STREAMS].bitcast(BF16))
-
-        def unit_front(unit):
-            x_bank = transposed_bank(rows[("x", unit)], 0, WORDS)
-            h_bank[unit] = transposed_bank(rows[("h", unit)], 0, WORDS)
-            c_bank = transposed_bank(rows[("c", unit)], 0, WORDS)
-            xh_grouped[unit] = work.tile([P, 2 * 4 * UNIT_ROWS], BF16, tag="xh_grouped", name="xh_grouped", align_bytes=64)
-            copy_grouped("scalar", xh_grouped[unit][:].bitcast(F32)[:, 0:BANK], x_bank)
+        def tanh_of(unit):
             tanh_c[unit] = slow.tile([P, 4 * UNIT_ROWS], F32, tag="tanh_c", name="tanh_c")
             nc.scalar.activation(
                 out=tanh_c[unit][:].rearrange("p (u e n) -> p u e n", u=2, e=2),
-                in_=c_bank[:].bitcast(BF16).rearrange("p (u n e) -> p u e n", u=2, e=2),
+                in_=turned_bank[("c", unit)][:].bitcast(BF16).rearrange("p (u n e) -> p u e n", u=2, e=2),
                 func=ACT.Tanh,
             )
 
-        def copy_h(unit):
-            copy_grouped("vector", xh_grouped[unit][:].bitcast(F32)[:, BANK : 2 * BANK], h_bank[unit])
+        def bias_o():
+            turned = psum_t.tile([P, BANK], F32, tag="turned", name="turned")
+            nc.tensor.transpose(turned[:, 0:P], bias_rows[:, STREAMS * OUTF :].bitcast(F32), ident[:])
+            nc.vector.tensor_copy(out=bo_cols[:], in_=turned[:, 0 : 2 * STREAMS].bitcast(BF16))
 
-        def quantise_xh(unit):
-            words = work.tile([P, 2 * UNIT_ROWS], U32, tag="xh_words", name="xh_words", align_bytes=64)
-            scales = work.tile([P, 2 * UNIT_ROWS], U8, tag="xh_scales", name="xh_scales", align_bytes=64)
-            quantise(xh_grouped[unit][:], words[:], scales[:])
-            xh_mx[unit] = (words, scales)
+        def bias_y():
+            for half in range(2):
+                spread = psum_t.tile([P, BANK], F32, tag="turned", name="turned")
+                cols = slice(half * BANK, (half + 1) * BANK)
+                nc.tensor.matmul(out=spread[:], lhsT=ones[:], rhs=bias_rows[:, cols], start=True, stop=True)
+                nc.vector.tensor_copy(out=by_all[:, cols], in_=spread[:])
 
-        def gate_of(unit):
+        def gate_pass_pair(z, unit, t, r0, n):
+            s, u, e = unit // PER_STREAM, t // 2, t % 2
+            words, scales = mx[unit]
+            for g in range(2):
+                w_words, w_scales = wo_mx[(s, 2 * u + g)]
+                lo = (XH // 4) + g * UNIT_ROWS + r0
+                nc.tensor.matmul_mx(
+                    out=z,
+                    lhsT=w_words[:, e * P : (e + 1) * P].bitcast(FP8X4),
+                    lhsT_scale=w_scales[:, e * P : (e + 1) * P],
+                    rhs=words[:, lo : lo + n].bitcast(FP8X4),
+                    rhs_scale=scales[:, lo : lo + n],
+                    start=(g == 0),
+                    stop=(g == 1),
+                )
+
+        def gate_bank(unit, b, n):
             s = unit // PER_STREAM
-            words, scales = xh_mx[unit]
-            gate[unit] = work.tile([P, 4 * UNIT_ROWS], F32, tag="gate", name="gate")
-            for u in range(2):
-                z = psum.tile([P, BANK], F32, tag="bank", name="z")
-                for e in range(2):
-                    for g in range(2):
-                        lo = wo_start(s, 2 * u + g) + e * P
-                        nc.tensor.matmul_mx(
-                            out=z[:, e * UNIT_ROWS : (e + 1) * UNIT_ROWS],
-                            lhsT=wo_words[:, lo : lo + P].bitcast(FP8X4),
-                            lhsT_scale=wo_scales[:, lo : lo + P],
-                            rhs=words[:, g * UNIT_ROWS : (g + 1) * UNIT_ROWS].bitcast(FP8X4),
-                            rhs_scale=scales[:, g * UNIT_ROWS : (g + 1) * UNIT_ROWS],
-                            start=(g == 0),
-                            stop=(g == 1),
-                        )
-                for e in range(2):
-                    t = 2 * u + e
-                    nc.scalar.activation(
-                        out=gate[unit][:, t * UNIT_ROWS : (t + 1) * UNIT_ROWS],
-                        in_=z[:, e * UNIT_ROWS : (e + 1) * UNIT_ROWS],
-                        func=ACT.Sigmoid,
-                        bias=bo_cols[:, 4 * s + t : 4 * s + t + 1],
-                    )
+            if unit not in gate:
+                gate[unit] = work.tile([P, 4 * UNIT_ROWS], F32, tag="gate", name="gate")
+            z = psum_z.tile([P, BANK], F32, tag="z", name="z")
+            tiles = [(t, r0) for r0 in range(0, UNIT_ROWS, n) for t in range(4)]
+            members = tiles[b * (BANK // n) : (b + 1) * (BANK // n)]
+            for i, (t, r0) in enumerate(members):
+                gate_pass_pair(z[:, i * n : (i + 1) * n], unit, t, r0, n)
+            for i, (t, r0) in enumerate(members):
+                nc.scalar.activation(
+                    out=gate[unit][:, t * UNIT_ROWS + r0 : t * UNIT_ROWS + r0 + n],
+                    in_=z[:, i * n : (i + 1) * n],
+                    func=ACT.Sigmoid,
+                    bias=bo_cols[:, 4 * s + t : 4 * s + t + 1],
+                )
 
-        def gating_product(unit):
-            h_grouped[unit] = work.tile([P, 4 * UNIT_ROWS], BF16, tag="h_grouped", name="h_grouped", align_bytes=64)
+        def gating_product(unit, r0, n):
+            part = slice(r0 // 4, (r0 + n) // 4)
+            dst = batch_of(unit + 2)[:, HN : HN + 4 * UNIT_ROWS]
             nc.vector.tensor_tensor(
-                out=h_grouped[unit][:].rearrange("p (c i t) -> p c t i", i=4, t=4),
-                in0=gate[unit][:].rearrange("p (t c i) -> p c t i", t=4, i=4),
-                in1=tanh_c[unit][:].rearrange("p (t c i) -> p c t i", t=4, i=4),
+                out=dst.rearrange("p (c i t) -> p c t i", i=4, t=4)[:, part],
+                in0=gate[unit][:].rearrange("p (t c i) -> p c t i", t=4, i=4)[:, part],
+                in1=tanh_c[unit][:].rearrange("p (t c i) -> p c t i", t=4, i=4)[:, part],
                 op=ALU.mult,
             )
 
-        def quantise_h(unit):
-            words = work.tile([P, UNIT_ROWS], U32, tag="h_words", name="h_words", align_bytes=64)
-            scales = work.tile([P, UNIT_ROWS], U8, tag="h_scales", name="h_scales", align_bytes=64)
-            quantise(h_grouped[unit][:], words[:], scales[:])
-            h_mx[unit] = (words, scales)
-
-        def projection(unit):
+        def projection(unit, js):
             cols = stream_columns(unit // PER_STREAM)
-            words, scales = h_mx[unit]
-            y_bank[unit] = psum.tile([P, BANK], F32, tag="bank", name="y")
-            for j in range(2):
+            words, scales = mx[unit + 2]
+            bank = psum_y.tile([P, BANK], F32, tag="y", name="y")
+            for j in js:
+                lo = HN // 4 + j * P
                 nc.tensor.matmul_mx(
-                    out=y_bank[unit][:, j * OUTF : (j + 1) * OUTF],
-                    lhsT=words[:, j * P : (j + 1) * P].bitcast(FP8X4),
-                    lhsT_scale=scales[:, j * P : (j + 1) * P],
+                    out=bank[:, j * OUTF : (j + 1) * OUTF],
+                    lhsT=words[:, lo : lo + P].bitcast(FP8X4),
+                    lhsT_scale=scales[:, lo : lo + P],
                     rhs=wy_words[:, cols].bitcast(FP8X4),
                     rhs_scale=wy_scales[:, cols],
                     start=True,
                     stop=True,
                 )
+                y_bank[(unit, j)] = bank
 
-        def add_bias_and_store(unit):
+        def add_bias_and_store(unit, j0, n):
             cols, r0 = stream_columns(unit // PER_STREAM), (unit % PER_STREAM) * UNIT_ROWS
             y = slow.tile([P, 2 * OUTF], F32, tag="y_sb", name="y_sb")
+            dst = y[:].rearrange("p (j m) -> p j m", j=2)[:, j0 : j0 + n]
             nc.vector.tensor_tensor(
-                out=y[:].rearrange("p (j m) -> p j m", j=2),
-                in0=y_bank[unit][:].rearrange("p (j m) -> p j m", j=2),
-                in1=by_all[:, cols].unsqueeze(1).to_broadcast([P, 2, OUTF]),
+                out=dst,
+                in0=y_bank[(unit, j0)][:].rearrange("p (j m) -> p j m", j=2)[:, j0 : j0 + n],
+                in1=by_all[:, cols].unsqueeze(1).to_broadcast([P, n, OUTF]),
                 op=ALU.add,
             )
             nc.sync.dma_start(
-                out=out[r0 : r0 + UNIT_ROWS, cols].rearrange("(p j) m -> p j m", j=2),
-                in_=y[:].rearrange("p (j m) -> p j m", j=2),
+                out=out[r0 : r0 + UNIT_ROWS, cols].rearrange("(p j) m -> p j m", j=2)[:, j0 : j0 + n],
+                in_=dst,
             )
 
+        load_rows("x", 0)
+        load_rows("h", 0)
         load_wo_half(0, 0)
+        load_rows("c", 0)
         load_wo_half(0, 1)
-        for unit in range(PREFETCH):
+        for unit in range(1, PREFETCH):
             load_for_unit(unit)
 
-        for step in range(-PER_STREAM, UNITS + 3):
-            following, k = step // PER_STREAM + 1, step % PER_STREAM
-            if step == 0:
-                gate_of(0)
-            if following < STREAMS:
-                wo_bank(following, k)
-            if 0 <= step + 1 < UNITS:
-                unit_front(step + 1)
-            if following < STREAMS and k == PER_STREAM - 1:
-                wy_bank(following)
-            if step == -2:
-                biases()
-            if 0 <= step - 3:
-                add_bias_and_store(step - 3)
-            if 0 <= step + 1 < UNITS:
-                copy_h(step + 1)
-            if 0 <= step - 1 < UNITS:
-                gating_product(step - 1)
-            if 0 <= step + 1 < UNITS:
-                quantise_xh(step + 1)
-            if 0 <= step - 1 < UNITS:
-                quantise_h(step - 1)
-            if following < STREAMS:
-                weights_quantise(following, k)
-            if 0 <= step + 1:
-                load_for_unit(step + 1 + PREFETCH)
-            if 0 < step < UNITS:
-                gate_of(step)
-            if 0 <= step - 2 < UNITS:
-                projection(step - 2)
+        turn_rows("x", 0)
+        copy_rows("vector", "x", 0)
+        turn_rows("h", 0)
+        copy_rows("scalar", "h", 0)
+        turn_wo(0, 0)
+        turn_wo(0, 1)
+        turn_rows("c", 0)
+        copy_wo("vector", 0, 0, -4)
+        copy_wo("scalar", 0, 1, -3)
+        tanh_of(0)
+        quantise_batch(0, XH, HN)
+        quantise_batch(-4, WB, BATCH)
+        quantise_batch(-3, WB, BATCH)
+        keep_wo(0, 0, -4)
+        keep_wo(0, 1, -3)
+        bias_o()
+        turn_wo(0, 2)
+        turn_wo(0, 3)
+        copy_wo("vector", 0, 2, -2)
+        copy_wo("scalar", 0, 3, -1)
+        turn_rows("x", 1)
+        turn_rows("h", 1)
+        copy_rows("scalar", "x", 1)
+        quantise_batch(-2, WB, BATCH)
+        quantise_batch(-1, WB, BATCH)
+        keep_wo(0, 2, -2)
+        keep_wo(0, 3, -1)
+        copy_rows("vector", "h", 1)
+        quantise_batch(1, XH, HN)
+        gate_bank(0, 0, UNIT_ROWS)
+        gate_bank(0, 1, UNIT_ROWS)
+        turn_rows("c", 1)
+        tanh_of(1)
+        gating_product(0, 0, UNIT_ROWS)
+        turn_wo(1, 0)
+        copy_wo("scalar", 1, 0, 1)
+        gate_bank(1, 0, UNIT_ROWS)
+        gate_bank(1, 1, UNIT_ROWS)
+        quantise_batch(1, WB, BATCH)
+        keep_wo(1, 0, 1)
+        load_for_unit(PREFETCH)
+
+        for step in range(1, UNITS):
+            s, k = step // PER_STREAM, step % PER_STREAM
+            has_next, has_wo = step + 1 < UNITS, s + 1 < STREAMS
+            if has_next:
+                turn_rows("x", step + 1)
+                turn_rows("h", step + 1)
+            if has_wo:
+                turn_wo(s + 1, k)
+            if has_next:
+                turn_rows("c", step + 1)
+            if step == 1 or k == 0:
+                turn(("wy", s), wy_raw[s], 0, WORDS)
+            if has_next:
+                copy_rows("scalar", "x", step + 1)
+            if has_wo:
+                copy_wo("scalar", s + 1, k, step + 1)
+            if has_next:
+                tanh_of(step + 1)
+            if step > 1:
+                gating_product(step - 1, 0, UNIT_ROWS)
+            if has_next:
+                copy_rows("scalar" if step >= 14 else "vector", "h", step + 1)
+            if step >= 3:
+                add_bias_and_store(step - 3, 0, 2)
+            if has_wo:
+                quantise_batch(step + 1, XH, BATCH)
+                keep_wo(s + 1, k, step + 1)
+            else:
+                if has_next:
+                    quantise_batch(step + 1, XH, HN)
+                quantise_batch(step + 1, HN, WB)
+            if step == 1 or k == 0:
+                copy_wy("scalar", s)
+                quantise_wy(s)
+            if step == 2:
+                bias_y()
+            load_for_unit(step + PREFETCH)
+            for b in range(2 if step > 1 else 0):
+                gate_bank(step, b, P if step == LAST else UNIT_ROWS)
+            if step >= 2:
+                projection(step - 2, (0, 1))
+
+        projection(LAST - 1, (0, 1))
+        add_bias_and_store(LAST - 2, 0, 2)
+        gating_product(LAST, 0, P)
+        add_bias_and_store(LAST - 1, 0, 2)
+        quantise_batch(LAST + 2, HN, HN + 4 * P)
+        projection(LAST, (0,))
+        gating_product(LAST, P, P)
+        add_bias_and_store(LAST, 0, 1)
+        quantise_batch(LAST + 2, HN + 4 * P, WB)
+        projection(LAST, (1,))
+        add_bias_and_store(LAST, 1, 1)

@@ -24,6 +24,7 @@ UNITS = STREAMS * PER_STREAM
 LAST = UNITS - 1
 WO_BANKS = 4
 PREFETCH = 6
+POOL_SHARE = 96
 
 XH, HN, WB = 0, 4 * BANK, 6 * BANK
 BATCH = 8 * BANK
@@ -41,9 +42,9 @@ def tile_flatlstm_pb_t_kernel(tc, modulation, h0, c_new, Wo, b_o, Wy, b_y, out):
         slow = ctx.enter_context(tc.tile_pool(name="slow", bufs=4))
         mx_pool = ctx.enter_context(tc.tile_pool(name="mx_pool", bufs=9))
         rows_pool = ctx.enter_context(tc.tile_pool(name="rows_pool", bufs=PREFETCH + 2))
-        psum_t = ctx.enter_context(tc.psum_pool(name="psum_t", bufs=4))
+        psum_t = ctx.enter_context(tc.psum_pool(name="psum_t", bufs=5))
         psum_z = ctx.enter_context(tc.psum_pool(name="psum_z", bufs=2))
-        psum_y = ctx.enter_context(tc.psum_pool(name="psum_y", bufs=2))
+        psum_y = ctx.enter_context(tc.psum_pool(name="psum_y", bufs=1))
         ctx.enter_context(tc.manual_schedule())
 
         bias_rows = const.tile([P, STREAMS * OUTF + 2 * P], BF16, name="bias_rows")
@@ -100,12 +101,13 @@ def tile_flatlstm_pb_t_kernel(tc, modulation, h0, c_new, Wo, b_o, Wy, b_y, out):
             if unit >= UNITS:
                 return
             s, k = unit // PER_STREAM, unit % PER_STREAM
+            first = 2 if s == 0 else 1
             for kind in ("x", "h", "c"):
                 load_rows(kind, unit)
-            if s + 1 < STREAMS and k % 2 == 1:
-                load_wo_half(s + 1, k // 2)
-            if k == 1:
+            if k == first:
                 load_wy(s)
+            if s + 1 < STREAMS and k in (first, 3):
+                load_wo_half(s + 1, k // 3)
 
         def batch_of(j):
             if j not in grouped:
@@ -221,10 +223,10 @@ def tile_flatlstm_pb_t_kernel(tc, modulation, h0, c_new, Wo, b_o, Wy, b_y, out):
                     bias=bo_cols[:, 4 * s + t : 4 * s + t + 1],
                 )
 
-        def gating_product(unit, r0, n):
+        def product_part(engine, unit, r0, n):
             part = slice(r0 // 4, (r0 + n) // 4)
             dst = batch_of(unit + 2)[:, HN : HN + 4 * UNIT_ROWS]
-            nc.vector.tensor_tensor(
+            engine.tensor_tensor(
                 out=dst.rearrange("p (c i t) -> p c t i", i=4, t=4)[:, part],
                 in0=gate[unit][:].rearrange("p (t c i) -> p c t i", t=4, i=4)[:, part],
                 in1=tanh_c[unit][:].rearrange("p (t c i) -> p c t i", t=4, i=4)[:, part],
@@ -234,7 +236,10 @@ def tile_flatlstm_pb_t_kernel(tc, modulation, h0, c_new, Wo, b_o, Wy, b_y, out):
         def projection(unit, js):
             cols = stream_columns(unit // PER_STREAM)
             words, scales = mx[unit + 2]
-            bank = psum_y.tile([P, BANK], F32, tag="y", name="y")
+            if unit < LAST - 1:
+                bank = psum_y.tile([P, BANK], F32, tag="y", name="y")
+            else:
+                bank = psum_t.tile([P, BANK], F32, tag="turned", name="y_last")
             for j in js:
                 lo = HN // 4 + j * P
                 nc.tensor.matmul_mx(
@@ -262,6 +267,13 @@ def tile_flatlstm_pb_t_kernel(tc, modulation, h0, c_new, Wo, b_o, Wy, b_y, out):
                 out=out[r0 : r0 + UNIT_ROWS, cols].rearrange("(p j) m -> p j m", j=2)[:, j0 : j0 + n],
                 in_=dst,
             )
+
+        def product_on_pool(unit, r0, n):
+            product_part(nc.gpsimd, unit, r0, n * POOL_SHARE // UNIT_ROWS)
+
+        def product_on_vector(unit, r0, n):
+            share = n * POOL_SHARE // UNIT_ROWS
+            product_part(nc.vector, unit, r0 + share, n - share)
 
         load_rows("x", 0)
         load_rows("h", 0)
@@ -304,65 +316,73 @@ def tile_flatlstm_pb_t_kernel(tc, modulation, h0, c_new, Wo, b_o, Wy, b_y, out):
         gate_bank(0, 1, UNIT_ROWS)
         turn_rows("c", 1)
         tanh_of(1)
-        gating_product(0, 0, UNIT_ROWS)
-        turn_wo(1, 0)
-        copy_wo("scalar", 1, 0, 1)
+        bias_y()
+        product_on_pool(0, 0, UNIT_ROWS)
+        product_on_vector(0, 0, UNIT_ROWS)
         gate_bank(1, 0, UNIT_ROWS)
         gate_bank(1, 1, UNIT_ROWS)
-        quantise_batch(1, WB, BATCH)
-        keep_wo(1, 0, 1)
         load_for_unit(PREFETCH)
 
-        for step in range(1, UNITS):
+        for step in range(1, LAST):
             s, k = step // PER_STREAM, step % PER_STREAM
-            has_next, has_wo = step + 1 < UNITS, s + 1 < STREAMS
-            if has_next:
-                turn_rows("x", step + 1)
-                turn_rows("h", step + 1)
+            has_wo = s + 1 < STREAMS
+            b = k - 1 if s == 0 else k
+            has_wy = step == 1 or k == 0
+            wo_engine = "vector" if k == 2 else "scalar"
+            turn_rows("x", step + 1)
+            turn_rows("h", step + 1)
             if has_wo:
-                turn_wo(s + 1, k)
-            if has_next:
-                turn_rows("c", step + 1)
-            if step == 1 or k == 0:
+                turn_wo(s + 1, b)
+            turn_rows("c", step + 1)
+            if has_wy:
                 turn(("wy", s), wy_raw[s], 0, WORDS)
-            if has_next:
-                copy_rows("scalar", "x", step + 1)
-            if has_wo:
-                copy_wo("scalar", s + 1, k, step + 1)
-            if has_next:
-                tanh_of(step + 1)
-            if step > 1:
-                gating_product(step - 1, 0, UNIT_ROWS)
-            if has_next:
-                copy_rows("scalar" if step >= 14 else "vector", "h", step + 1)
+            copy_rows("scalar", "x", step + 1)
+            if has_wo and wo_engine == "scalar":
+                copy_wo("scalar", s + 1, b, step + 1)
+            tanh_of(step + 1)
+            product = None if step == 2 else 1 if step == 1 else step - 1
+            if product is not None:
+                product_on_pool(product, 0, UNIT_ROWS)
             if step >= 3:
                 add_bias_and_store(step - 3, 0, 2)
+            copy_rows("scalar" if step == LAST - 1 else "vector", "h", step + 1)
+            if has_wo and wo_engine == "vector":
+                copy_wo("vector", s + 1, b, step + 1)
+            if product is not None:
+                product_on_vector(product, 0, UNIT_ROWS)
+            quantise_batch(step + 1, XH, HN)
+            quantise_batch(step + 1, HN, BATCH if has_wo else WB)
             if has_wo:
-                quantise_batch(step + 1, XH, BATCH)
-                keep_wo(s + 1, k, step + 1)
-            else:
-                if has_next:
-                    quantise_batch(step + 1, XH, HN)
-                quantise_batch(step + 1, HN, WB)
-            if step == 1 or k == 0:
+                keep_wo(s + 1, b, step + 1)
+            if has_wy:
                 copy_wy("scalar", s)
                 quantise_wy(s)
-            if step == 2:
-                bias_y()
+            if step == 3:
+                turn_wo(1, 3)
+                copy_wo("vector", 1, 3, -5)
+                quantise_batch(-5, WB, BATCH)
+                keep_wo(1, 3, -5)
             load_for_unit(step + PREFETCH)
-            for b in range(2 if step > 1 else 0):
-                gate_bank(step, b, P if step == LAST else UNIT_ROWS)
-            if step >= 2:
+            if step > 1:
+                gate_bank(step, 0, UNIT_ROWS)
+                gate_bank(step, 1, UNIT_ROWS)
                 projection(step - 2, (0, 1))
 
+        product_on_pool(LAST - 1, 0, UNIT_ROWS)
+        add_bias_and_store(LAST - 3, 0, 2)
+        product_on_vector(LAST - 1, 0, UNIT_ROWS)
+        gate_bank(LAST, 0, P)
+        gate_bank(LAST, 1, P)
+        projection(LAST - 2, (0, 1))
+        product_part(nc.vector, LAST, 0, P)
+        quantise_batch(LAST + 1, HN, WB)
         projection(LAST - 1, (0, 1))
-        add_bias_and_store(LAST - 2, 0, 2)
-        gating_product(LAST, 0, P)
-        add_bias_and_store(LAST - 1, 0, 2)
+        product_part(nc.vector, LAST, P, P)
         quantise_batch(LAST + 2, HN, HN + 4 * P)
         projection(LAST, (0,))
-        gating_product(LAST, P, P)
-        add_bias_and_store(LAST, 0, 1)
+        add_bias_and_store(LAST - 2, 0, 2)
         quantise_batch(LAST + 2, HN + 4 * P, WB)
         projection(LAST, (1,))
+        add_bias_and_store(LAST - 1, 0, 2)
+        add_bias_and_store(LAST, 0, 1)
         add_bias_and_store(LAST, 1, 1)

@@ -215,7 +215,7 @@ def tile_flatlstm_pb_t_kernel(tc, modulation, h0, c_new, Wo, b_o, Wy, b_y, out):
             members = tiles[b * (BANK // n) : (b + 1) * (BANK // n)]
             for i, (t, r0) in enumerate(members):
                 gate_pass_pair(z[:, i * n : (i + 1) * n], unit, t, r0, n)
-            for i, (t, r0) in enumerate(members):
+            for i, (t, r0) in reversed(list(enumerate(members))):
                 nc.scalar.activation(
                     out=gate[unit][:, t * UNIT_ROWS + r0 : t * UNIT_ROWS + r0 + n],
                     in_=z[:, i * n : (i + 1) * n],
@@ -345,7 +345,7 @@ def tile_flatlstm_pb_t_kernel(tc, modulation, h0, c_new, Wo, b_o, Wy, b_y, out):
                 product_on_pool(product, 0, UNIT_ROWS)
             if step >= 3:
                 add_bias_and_store(step - 3, 0, 2)
-            copy_rows("scalar" if step == LAST - 1 else "vector", "h", step + 1)
+            copy_rows("vector", "h", step + 1)
             if has_wo and wo_engine == "vector":
                 copy_wo("vector", s + 1, b, step + 1)
             if product is not None:

@@ -47,6 +47,8 @@ def tile_flatlstm_pb_t_kernel(tc, modulation, h0, c_new, Wo, b_o, Wy, b_y, out):
         psum_y = ctx.enter_context(tc.psum_pool(name="psum_y", bufs=1))
         ctx.enter_context(tc.manual_schedule())
 
+        ones = const.tile([P, BANK], BF16, name="ones")
+        nc.vector.memset(ones[:], 1.0)
         bias_rows = const.tile([P, STREAMS * OUTF + 2 * P], BF16, name="bias_rows")
         nc.vector.memset(bias_rows[:].bitcast(I32), 0)
         nc.scalar.dma_start(out=bias_rows[0:1, 0 : STREAMS * OUTF], in_=b_y.rearrange("(o s) m -> o (s m)", o=1))
@@ -59,8 +61,6 @@ def tile_flatlstm_pb_t_kernel(tc, modulation, h0, c_new, Wo, b_o, Wy, b_y, out):
         nc.scalar.activation(out=warm_out[:], in_=warm_in[:], func=ACT.Sigmoid)
         ident = const.tile([P, P], F32, name="ident")
         make_identity(nc, ident[:])
-        ones = const.tile([P, P], BF16, name="ones")
-        nc.vector.memset(ones[:], 1.0)
 
         wy_words = const.tile([P, STREAMS * OUTF], U32, name="wy_words", align_bytes=64)
         wy_scales = const.tile([P, STREAMS * OUTF], U8, name="wy_scales", align_bytes=64)
@@ -187,7 +187,7 @@ def tile_flatlstm_pb_t_kernel(tc, modulation, h0, c_new, Wo, b_o, Wy, b_y, out):
             for half in range(2):
                 spread = psum_t.tile([P, BANK], F32, tag="turned", name="turned")
                 cols = slice(half * BANK, (half + 1) * BANK)
-                nc.tensor.matmul(out=spread[:], lhsT=ones[:], rhs=bias_rows[:, cols], start=True, stop=True)
+                nc.tensor.matmul(out=spread[:], lhsT=ones[:, 0:P], rhs=bias_rows[:, cols], start=True, stop=True)
                 nc.vector.tensor_copy(out=by_all[:, cols], in_=spread[:])
 
         def gate_pass_pair(z, unit, t, r0, n):
@@ -275,6 +275,12 @@ def tile_flatlstm_pb_t_kernel(tc, modulation, h0, c_new, Wo, b_o, Wy, b_y, out):
             share = n * POOL_SHARE // UNIT_ROWS
             product_part(nc.vector, unit, r0 + share, n - share)
 
+        idle_bank = psum_z.tile([P, BANK], F32, tag="z", name="idle_bank")
+
+        def keep_busy(count):
+            for i in range(count):
+                nc.tensor.matmul(out=idle_bank[:], lhsT=ones[:, 0:P], rhs=ones[:], start=True, stop=True)
+
         load_rows("x", 0)
         load_rows("h", 0)
         load_wo_half(0, 0)
@@ -283,13 +289,16 @@ def tile_flatlstm_pb_t_kernel(tc, modulation, h0, c_new, Wo, b_o, Wy, b_y, out):
         for unit in range(1, PREFETCH):
             load_for_unit(unit)
 
+        keep_busy(5)
         turn_rows("x", 0)
         copy_rows("vector", "x", 0)
         turn_rows("h", 0)
+        keep_busy(2)
         copy_rows("scalar", "h", 0)
         turn_wo(0, 0)
         turn_wo(0, 1)
         turn_rows("c", 0)
+        keep_busy(2)
         copy_wo("vector", 0, 0, -4)
         copy_wo("scalar", 0, 1, -3)
         tanh_of(0)
@@ -305,6 +314,7 @@ def tile_flatlstm_pb_t_kernel(tc, modulation, h0, c_new, Wo, b_o, Wy, b_y, out):
         copy_wo("scalar", 0, 3, -1)
         turn_rows("x", 1)
         turn_rows("h", 1)
+        keep_busy(2)
         copy_rows("scalar", "x", 1)
         quantise_batch(-2, WB, BATCH)
         quantise_batch(-1, WB, BATCH)

@@ -23,7 +23,7 @@ PER_STREAM = ROWS // UNIT_ROWS
 UNITS = STREAMS * PER_STREAM
 LAST = UNITS - 1
 WO_BANKS = 4
-PREFETCH = 6
+PREFETCH = 8
 POOL_SHARE = 96
 
 XH, HN, WB = 0, 4 * BANK, 6 * BANK
@@ -36,10 +36,11 @@ def tile_flatlstm_pb_t_kernel(tc, modulation, h0, c_new, Wo, b_o, Wy, b_y, out):
     nc = tc.nc
     with ExitStack() as ctx:
         const = ctx.enter_context(tc.tile_pool(name="const", bufs=1))
-        wo_pool = ctx.enter_context(tc.tile_pool(name="wo_pool", bufs=6))
-        wy_pool = ctx.enter_context(tc.tile_pool(name="wy_pool", bufs=2))
+        wo_pool = ctx.enter_context(tc.tile_pool(name="wo_pool", bufs=8))
+        wy_pool = ctx.enter_context(tc.tile_pool(name="wy_pool", bufs=4))
         work = ctx.enter_context(tc.tile_pool(name="work", bufs=3))
         slow = ctx.enter_context(tc.tile_pool(name="slow", bufs=4))
+        y_pool = ctx.enter_context(tc.tile_pool(name="y_pool", bufs=7))
         mx_pool = ctx.enter_context(tc.tile_pool(name="mx_pool", bufs=9))
         rows_pool = ctx.enter_context(tc.tile_pool(name="rows_pool", bufs=PREFETCH + 2))
         psum_t = ctx.enter_context(tc.psum_pool(name="psum_t", bufs=5))
@@ -145,7 +146,7 @@ def tile_flatlstm_pb_t_kernel(tc, modulation, h0, c_new, Wo, b_o, Wy, b_y, out):
             copy_grouped(engine, ("wo", s, b), batch_of(j)[:, WB : WB + 2 * BANK].bitcast(F32))
 
         def copy_wy(engine, s):
-            wy_grouped[s] = wy_pool.tile([P, 2 * BANK], BF16, tag="wy_grouped", name="wy_grouped", align_bytes=64)
+            wy_grouped[s] = work.tile([P, 2 * BANK], BF16, tag="wy_grouped", name="wy_grouped", align_bytes=64)
             copy_grouped(engine, ("wy", s), wy_grouped[s][:].bitcast(F32))
 
         def quantise(words, scales, values):
@@ -255,7 +256,7 @@ def tile_flatlstm_pb_t_kernel(tc, modulation, h0, c_new, Wo, b_o, Wy, b_y, out):
 
         def add_bias_and_store(unit, j0, n):
             cols, r0 = stream_columns(unit // PER_STREAM), (unit % PER_STREAM) * UNIT_ROWS
-            y = slow.tile([P, 2 * OUTF], F32, tag="y_sb", name="y_sb")
+            y = y_pool.tile([P, 2 * OUTF], F32, tag="y_sb", name="y_sb")
             dst = y[:].rearrange("p (j m) -> p j m", j=2)[:, j0 : j0 + n]
             nc.vector.tensor_tensor(
                 out=dst,

@@ -24,7 +24,7 @@ UNITS = STREAMS * PER_STREAM
 LAST = UNITS - 1
 WO_BANKS = 4
 PREFETCH = 8
-POOL_SHARE = 96
+POOL_SHARE = 128
 
 XH, HN, WB = 0, 4 * BANK, 6 * BANK
 BATCH = 8 * BANK

@@ -339,7 +339,7 @@ def tile_flatlstm_pb_t_kernel(tc, modulation, h0, c_new, Wo, b_o, Wy, b_y, out):
             has_wo = s + 1 < STREAMS
             b = k - 1 if s == 0 else k
             has_wy = step == 1 or k == 0
-            wo_engine = "vector" if k == 2 else "scalar"
+            wo_engine = "vector" if k % 2 == 0 else "scalar"
             turn_rows("x", step + 1)
             turn_rows("h", step + 1)
             if has_wo:
@@ -370,18 +370,18 @@ def tile_flatlstm_pb_t_kernel(tc, modulation, h0, c_new, Wo, b_o, Wy, b_y, out):
                 quantise_wy(s)
             if step == 3:
                 turn_wo(1, 3)
-                copy_wo("vector", 1, 3, -5)
+                copy_wo("scalar", 1, 3, -5)
                 quantise_batch(-5, WB, BATCH)
                 keep_wo(1, 3, -5)
             load_for_unit(step + PREFETCH)
             if step > 1:
-                gate_bank(step, 0, UNIT_ROWS)
-                gate_bank(step, 1, UNIT_ROWS)
+                for bank in range(2):
+                    gate_bank(step, bank, P if step == LAST - 1 else UNIT_ROWS)
                 projection(step - 2, (0, 1))
 
-        product_on_pool(LAST - 1, 0, UNIT_ROWS)
+        product_part(nc.vector, LAST - 1, 0, P)
         add_bias_and_store(LAST - 3, 0, 2)
-        product_on_vector(LAST - 1, 0, UNIT_ROWS)
+        product_part(nc.vector, LAST - 1, P, P)
         gate_bank(LAST, 0, P)
         gate_bank(LAST, 1, P)
         projection(LAST - 2, (0, 1))

from contextlib import ExitStack

import concourse.mybir as mybir
from concourse.masks import make_identity

F32 = mybir.dt.float32
BF16 = mybir.dt.bfloat16
U32 = mybir.dt.uint32
U8 = mybir.dt.uint8
I32 = mybir.dt.int32
FP8X4 = mybir.dt.float8_e4m3fn_x4
ACT = mybir.ActivationFunctionType
ALU = mybir.AluOpType

P = 128
ROWS, STREAMS = 1024, 4
FEAT = 512
OUTF = 256
WORDS = FEAT // 2
BANK = 512
UNIT_ROWS = 256
PER_STREAM = ROWS // UNIT_ROWS
UNITS = STREAMS * PER_STREAM
LAST = UNITS - 1
WO_BANKS = 4
PREFETCH = 8
POOL_SHARE = 128

XH, HN, WB = 0, 4 * BANK, 6 * BANK
BATCH = 8 * BANK

FLOPS = 2 * ROWS * STREAMS * (2 * FEAT * FEAT + FEAT * OUTF)


def tile_flatlstm_pb_t_kernel(tc, modulation, h0, c_new, Wo, b_o, Wy, b_y, out):
    nc = tc.nc
    with ExitStack() as ctx:
        const = ctx.enter_context(tc.tile_pool(name="const", bufs=1))
        wo_pool = ctx.enter_context(tc.tile_pool(name="wo_pool", bufs=8))
        wy_pool = ctx.enter_context(tc.tile_pool(name="wy_pool", bufs=4))
        work = ctx.enter_context(tc.tile_pool(name="work", bufs=3))
        slow = ctx.enter_context(tc.tile_pool(name="slow", bufs=4))
        y_pool = ctx.enter_context(tc.tile_pool(name="y_pool", bufs=7))
        mx_pool = ctx.enter_context(tc.tile_pool(name="mx_pool", bufs=9))
        rows_pool = ctx.enter_context(tc.tile_pool(name="rows_pool", bufs=PREFETCH + 2))
        psum_t = ctx.enter_context(tc.psum_pool(name="psum_t", bufs=5))
        psum_z = ctx.enter_context(tc.psum_pool(name="psum_z", bufs=2))
        psum_y = ctx.enter_context(tc.psum_pool(name="psum_y", bufs=1))
        ctx.enter_context(tc.manual_schedule())

        ones = const.tile([P, BANK], BF16, name="ones")
        nc.vector.memset(ones[:], 1.0)
        bias_rows = const.tile([P, STREAMS * OUTF + 2 * P], BF16, name="bias_rows")
        nc.vector.memset(bias_rows[:].bitcast(I32), 0)
        nc.scalar.dma_start(out=bias_rows[0:1, 0 : STREAMS * OUTF], in_=b_y.rearrange("(o s) m -> o (s m)", o=1))
        nc.scalar.dma_start(
            out=bias_rows[0 : 2 * STREAMS, STREAMS * OUTF :], in_=b_o.rearrange("s (u q) -> (s u) q", u=2)
        )
        warm_in = const.tile([P, 1], F32, name="warm_in")
        warm_out = const.tile([P, 1], F32, name="warm_out")
        nc.vector.memset(warm_in[:], 0.0)
        nc.scalar.activation(out=warm_out[:], in_=warm_in[:], func=ACT.Sigmoid)
        ident = const.tile([P, P], F32, name="ident")
        make_identity(nc, ident[:])

        wy_words = const.tile([P, STREAMS * OUTF], U32, name="wy_words", align_bytes=64)
        wy_scales = const.tile([P, STREAMS * OUTF], U8, name="wy_scales", align_bytes=64)
        by_all = const.tile([P, STREAMS * OUTF], F32, name="by_all")
        bo_cols = const.tile([P, 4 * STREAMS], F32, name="bo_cols")

        sources = {"x": modulation, "h": h0, "c": c_new}
        rows = {}
        wo_raw = {}
        wy_raw = {}
        grouped = {}
        mx = {}
        wo_mx = {}
        wy_grouped, tanh_c, gate, y_bank, turned_bank = {}, {}, {}, {}, {}

        def load_rows(kind, unit):
            s, r0 = unit // PER_STREAM, (unit % PER_STREAM) * UNIT_ROWS
            t = rows_pool.tile([P, 2 * FEAT], BF16, tag="rows_" + kind, name="rows_" + kind)
            nc.sync.dma_start(
                out=t[:].rearrange("p (j d) -> p j d", j=2),
                in_=sources[kind][r0 : r0 + UNIT_ROWS, s * FEAT : (s + 1) * FEAT].rearrange("(p j) d -> p j d", j=2),
            )
            rows[(kind, unit)] = t[:].bitcast(F32)

        def load_wo_half(s, u):
            t = wo_pool.tile([P, 4 * FEAT], BF16, tag="wo_raw", name="wo_raw")
            nc.sync.dma_start(out=t[:], in_=Wo[s][u * 2 * P : (u + 1) * 2 * P, :].rearrange("(p e) d -> p (e d)", e=2))
            wo_raw[(s, u)] = t[:].bitcast(F32)

        def load_wy(s):
            t = wy_pool.tile([P, 2 * FEAT], BF16, tag="wy_raw", name="wy_raw")
            nc.sync.dma_start(
                out=t[:].rearrange("p (j l) -> p j l", j=2), in_=Wy[s].rearrange("(j p) l -> p j l", j=2)
            )
            wy_raw[s] = t[:].bitcast(F32)

        def load_for_unit(unit):
            if unit >= UNITS:
                return
            s, k = unit // PER_STREAM, unit % PER_STREAM
            first = 2 if s == 0 else 1
            for kind in ("x", "h", "c"):
                load_rows(kind, unit)
            if k == first:
                load_wy(s)
            if s + 1 < STREAMS and k in (first, 3):
                load_wo_half(s + 1, k // 3)

        def batch_of(j):
            if j not in grouped:
                grouped[j] = work.tile([P, BATCH], BF16, tag="grouped", name="grouped", align_bytes=64)
            return grouped[j]

        def turn(key, words, base, row_step):
            bank = psum_t.tile([P, BANK], F32, tag="turned", name="turned")
            for u in range(2):
                for j in range(2):
                    lo = base + j * row_step + u * P
                    q = 2 * u + j
                    nc.tensor.transpose(bank[:, q * P : (q + 1) * P], words[:, lo : lo + P], ident[:])
            turned_bank[key] = bank

        def copy_grouped(engine, key, grouped_words):
            dst = grouped_words.rearrange("p (n u) -> p n u", u=2)
            src = turned_bank[key][:].rearrange("p (u n) -> p n u", u=2)
            if engine == "scalar":
                nc.scalar.copy(out=dst, in_=src)
            else:
                nc.vector.tensor_copy(out=dst, in_=src)

        def turn_rows(kind, unit):
            turn((kind, unit), rows[(kind, unit)], 0, WORDS)

        def turn_wo(s, b):
            turn(("wo", s, b), wo_raw[(s, b // 2)], (b % 2) * WORDS, 2 * WORDS)

        def copy_rows(engine, kind, unit):
            lo = XH + (0 if kind == "x" else 2 * BANK)
            copy_grouped(engine, (kind, unit), batch_of(unit)[:, lo : lo + 2 * BANK].bitcast(F32))

        def copy_wo(engine, s, b, j):
            copy_grouped(engine, ("wo", s, b), batch_of(j)[:, WB : WB + 2 * BANK].bitcast(F32))

        def copy_wy(engine, s):
            wy_grouped[s] = work.tile([P, 2 * BANK], BF16, tag="wy_grouped", name="wy_grouped", align_bytes=64)
            copy_grouped(engine, ("wy", s), wy_grouped[s][:].bitcast(F32))

        def quantise(words, scales, values):
            nc.vector.quantize_mx(out=words.bitcast(FP8X4), scales=scales, in_=values)

        def quantise_batch(j, lo, hi):
            if j not in mx:
                words = mx_pool.tile([P, BATCH // 4], U32, tag="mx_words", name="mx_words", align_bytes=64)
                scales = mx_pool.tile([P, BATCH // 4], U8, tag="mx_scales", name="mx_scales", align_bytes=64)
                mx[j] = (words, scales)
            words, scales = mx[j]
            quantise(words[:, lo // 4 : hi // 4], scales[:, lo // 4 : hi // 4], grouped[j][:, lo:hi])

        def keep_wo(s, b, j):
            cols = slice(WB // 4, BATCH // 4)
            wo_mx[(s, b)] = (mx[j][0][:, cols], mx[j][1][:, cols])

        def stream_columns(s):
            return slice(s * OUTF, (s + 1) * OUTF)

        def quantise_wy(s):
            cols = stream_columns(s)
            quantise(wy_words[:, cols], wy_scales[:, cols], wy_grouped[s][:])

        def tanh_of(unit):
            tanh_c[unit] = slow.tile([P, 4 * UNIT_ROWS], F32, tag="tanh_c", name="tanh_c")
            nc.scalar.activation(
                out=tanh_c[unit][:].rearrange("p (u e n) -> p u e n", u=2, e=2),
                in_=turned_bank[("c", unit)][:].bitcast(BF16).rearrange("p (u n e) -> p u e n", u=2, e=2),
                func=ACT.Tanh,
            )

        def bias_o():
            turned = psum_t.tile([P, BANK], F32, tag="turned", name="turned")
            nc.tensor.transpose(turned[:, 0:P], bias_rows[:, STREAMS * OUTF :].bitcast(F32), ident[:])
            nc.vector.tensor_copy(out=bo_cols[:], in_=turned[:, 0 : 2 * STREAMS].bitcast(BF16))

        def bias_y():
            for half in range(2):
                spread = psum_t.tile([P, BANK], F32, tag="turned", name="turned")
                cols = slice(half * BANK, (half + 1) * BANK)
                nc.tensor.matmul(out=spread[:], lhsT=ones[:, 0:P], rhs=bias_rows[:, cols], start=True, stop=True)
                nc.vector.tensor_copy(out=by_all[:, cols], in_=spread[:])

        def gate_pass_pair(z, unit, t, r0, n):
            s, u, e = unit // PER_STREAM, t // 2, t % 2
            words, scales = mx[unit]
            for g in range(2):
                w_words, w_scales = wo_mx[(s, 2 * u + g)]
                lo = (XH // 4) + g * UNIT_ROWS + r0
                nc.tensor.matmul_mx(
                    out=z,
                    lhsT=w_words[:, e * P : (e + 1) * P].bitcast(FP8X4),
                    lhsT_scale=w_scales[:, e * P : (e + 1) * P],
                    rhs=words[:, lo : lo + n].bitcast(FP8X4),
                    rhs_scale=scales[:, lo : lo + n],
                    start=(g == 0),
                    stop=(g == 1),
                )

        def gate_bank(unit, b, n):
            s = unit // PER_STREAM
            if unit not in gate:
                gate[unit] = work.tile([P, 4 * UNIT_ROWS], F32, tag="gate", name="gate")
            z = psum_z.tile([P, BANK], F32, tag="z", name="z")
            tiles = [(t, r0) for r0 in range(0, UNIT_ROWS, n) for t in range(4)]
            members = tiles[b * (BANK // n) : (b + 1) * (BANK // n)]
            for i, (t, r0) in enumerate(members):
                gate_pass_pair(z[:, i * n : (i + 1) * n], unit, t, r0, n)
            for i, (t, r0) in reversed(list(enumerate(members))):
                nc.scalar.activation(
                    out=gate[unit][:, t * UNIT_ROWS + r0 : t * UNIT_ROWS + r0 + n],
                    in_=z[:, i * n : (i + 1) * n],
                    func=ACT.Sigmoid,
                    bias=bo_cols[:, 4 * s + t : 4 * s + t + 1],
                )

        def product_part(engine, unit, r0, n):
            part = slice(r0 // 4, (r0 + n) // 4)
            dst = batch_of(unit + 2)[:, HN : HN + 4 * UNIT_ROWS]
            engine.tensor_tensor(
                out=dst.rearrange("p (c i t) -> p c t i", i=4, t=4)[:, part],
                in0=gate[unit][:].rearrange("p (t c i) -> p c t i", t=4, i=4)[:, part],
                in1=tanh_c[unit][:].rearrange("p (t c i) -> p c t i", t=4, i=4)[:, part],
                op=ALU.mult,
            )

        def projection(unit, js):
            cols = stream_columns(unit // PER_STREAM)
            words, scales = mx[unit + 2]
            if unit < LAST - 1:
                bank = psum_y.tile([P, BANK], F32, tag="y", name="y")
            else:
                bank = psum_t.tile([P, BANK], F32, tag="turned", name="y_last")
            for j in js:
                lo = HN // 4 + j * P
                nc.tensor.matmul_mx(
                    out=bank[:, j * OUTF : (j + 1) * OUTF],
                    lhsT=words[:, lo : lo + P].bitcast(FP8X4),
                    lhsT_scale=scales[:, lo : lo + P],
                    rhs=wy_words[:, cols].bitcast(FP8X4),
                    rhs_scale=wy_scales[:, cols],
                    start=True,
                    stop=True,
                )
                y_bank[(unit, j)] = bank

        def add_bias_and_store(unit, j0, n):
            cols, r0 = stream_columns(unit // PER_STREAM), (unit % PER_STREAM) * UNIT_ROWS
            y = y_pool.tile([P, 2 * OUTF], F32, tag="y_sb", name="y_sb")
            dst = y[:].rearrange("p (j m) -> p j m", j=2)[:, j0 : j0 + n]
            nc.vector.tensor_tensor(
                out=dst,
                in0=y_bank[(unit, j0)][:].rearrange("p (j m) -> p j m", j=2)[:, j0 : j0 + n],
                in1=by_all[:, cols].unsqueeze(1).to_broadcast([P, n, OUTF]),
                op=ALU.add,
            )
            nc.sync.dma_start(
                out=out[r0 : r0 + UNIT_ROWS, cols].rearrange("(p j) m -> p j m", j=2)[:, j0 : j0 + n],
                in_=dst,
            )

        def product_on_pool(unit, r0, n):
            product_part(nc.gpsimd, unit, r0, n * POOL_SHARE // UNIT_ROWS)

        def product_on_vector(unit, r0, n):
            share = n * POOL_SHARE // UNIT_ROWS
            product_part(nc.vector, unit, r0 + share, n - share)

        idle_bank = psum_z.tile([P, BANK], F32, tag="z", name="idle_bank")

        def keep_busy(count):
            for i in range(count):
                nc.tensor.matmul(out=idle_bank[:], lhsT=ones[:, 0:P], rhs=ones[:], start=True, stop=True)

        load_rows("x", 0)
        load_rows("h", 0)
        load_wo_half(0, 0)
        load_rows("c", 0)
        load_wo_half(0, 1)
        for unit in range(1, PREFETCH):
            load_for_unit(unit)

        keep_busy(5)
        turn_rows("x", 0)
        copy_rows("vector", "x", 0)
        turn_rows("h", 0)
        keep_busy(2)
        copy_rows("scalar", "h", 0)
        turn_wo(0, 0)
        turn_wo(0, 1)
        turn_rows("c", 0)
        keep_busy(2)
        copy_wo("vector", 0, 0, -4)
        copy_wo("scalar", 0, 1, -3)
        tanh_of(0)
        quantise_batch(0, XH, HN)
        quantise_batch(-4, WB, BATCH)
        quantise_batch(-3, WB, BATCH)
        keep_wo(0, 0, -4)
        keep_wo(0, 1, -3)
        bias_o()
        turn_wo(0, 2)
        turn_wo(0, 3)
        copy_wo("vector", 0, 2, -2)
        copy_wo("scalar", 0, 3, -1)
        turn_rows("x", 1)
        turn_rows("h", 1)
        keep_busy(2)
        copy_rows("scalar", "x", 1)
        quantise_batch(-2, WB, BATCH)
        quantise_batch(-1, WB, BATCH)
        keep_wo(0, 2, -2)
        keep_wo(0, 3, -1)
        copy_rows("vector", "h", 1)
        quantise_batch(1, XH, HN)
        gate_bank(0, 0, UNIT_ROWS)
        gate_bank(0, 1, UNIT_ROWS)
        turn_rows("c", 1)
        tanh_of(1)
        bias_y()
        product_on_pool(0, 0, UNIT_ROWS)
        product_on_vector(0, 0, UNIT_ROWS)
        gate_bank(1, 0, UNIT_ROWS)
        gate_bank(1, 1, UNIT_ROWS)
        load_for_unit(PREFETCH)

        for step in range(1, LAST):
            s, k = step // PER_STREAM, step % PER_STREAM
            has_wo = s + 1 < STREAMS
            b = k - 1 if s == 0 else k
            has_wy = step == 1 or k == 0
            wo_engine = "vector" if k % 2 == 0 else "scalar"
            turn_rows("x", step + 1)
            turn_rows("h", step + 1)
            if has_wo:
                turn_wo(s + 1, b)
            turn_rows("c", step + 1)
            if has_wy:
                turn(("wy", s), wy_raw[s], 0, WORDS)
            copy_rows("scalar", "x", step + 1)
            if has_wo and wo_engine == "scalar":
                copy_wo("scalar", s + 1, b, step + 1)
            tanh_of(step + 1)
            product = None if step == 2 else 1 if step == 1 else step - 1
            if product is not None:
                product_on_pool(product, 0, UNIT_ROWS)
            if step >= 3:
                add_bias_and_store(step - 3, 0, 2)
            copy_rows("vector", "h", step + 1)
            if has_wo and wo_engine == "vector":
                copy_wo("vector", s + 1, b, step + 1)
            if product is not None:
                product_on_vector(product, 0, UNIT_ROWS)
            quantise_batch(step + 1, XH, HN)
            quantise_batch(step + 1, HN, BATCH if has_wo else WB)
            if has_wo:
                keep_wo(s + 1, b, step + 1)
            if has_wy:
                copy_wy("scalar", s)
                quantise_wy(s)
            if step == 3:
                turn_wo(1, 3)
                copy_wo("scalar", 1, 3, -5)
                quantise_batch(-5, WB, BATCH)
                keep_wo(1, 3, -5)
            load_for_unit(step + PREFETCH)
            if step > 1:
                for bank in range(2):
                    gate_bank(step, bank, P if step == LAST - 1 else UNIT_ROWS)
                projection(step - 2, (0, 1))

        product_part(nc.vector, LAST - 1, 0, P)
        add_bias_and_store(LAST - 3, 0, 2)
        product_part(nc.vector, LAST - 1, P, P)
        gate_bank(LAST, 0, P)
        gate_bank(LAST, 1, P)
        projection(LAST - 2, (0, 1))
        product_part(nc.vector, LAST, 0, P)
        quantise_batch(LAST + 1, HN, WB)
        projection(LAST - 1, (0, 1))
        product_part(nc.vector, LAST, P, P)
        quantise_batch(LAST + 2, HN, HN + 4 * P)
        projection(LAST, (0,))
        add_bias_and_store(LAST - 2, 0, 2)
        quantise_batch(LAST + 2, HN + 4 * P, WB)
        projection(LAST, (1,))
        add_bias_and_store(LAST - 1, 0, 2)
        add_bias_and_store(LAST, 0, 1)
        add_bias_and_store(LAST, 1, 1)
